import numpy as np
import ml_dtypes


def mxq(x, axis, fmt="e4m3"):
    dtype, down = {"e4m3": (ml_dtypes.float8_e4m3fn, 7), "e5m2": (ml_dtypes.float8_e5m2, 14)}[fmt]
    v = np.moveaxis(np.asarray(x, np.float32).astype(ml_dtypes.bfloat16).astype(np.float64), axis, -1)
    blocks = v.reshape(v.shape[:-1] + (-1, 32))
    amax = np.abs(blocks).max(-1, keepdims=True)
    byte = np.maximum(np.where(amax > 0, np.frexp(amax)[1] - 1 + 127, 0) - down, 1)
    scale = np.exp2(byte - 127.0)
    codes = (blocks / scale).astype(np.float32).astype(dtype).astype(np.float64)
    return np.moveaxis((codes * scale).reshape(v.shape), -1, axis)


WIDE = False


def mx_kscale(k):
    if not WIDE:
        return np.ones(k)
    levels = np.array([10, -10, 5, -5, 0])
    a = np.random.permutation(np.resize(levels, k // 512 * 4)).reshape(k // 512, 4)
    idx = np.arange(k)
    return np.exp2(a[idx // 512, idx % 128 // 32])


BF16 = ml_dtypes.bfloat16


def bf(x):
    return np.asarray(x, np.float32).astype(BF16)


def f64(x):
    return np.asarray(x).astype(np.float64)


N, D, O, H, W = 4, 512, 512, 32, 32
K = D + D
P = H * W


def exp_softmax_pool(y):
    a = np.exp(y)
    e = np.exp(a - a.max(-1, keepdims=True))
    sm = e / e.sum(-1, keepdims=True)
    return (sm * y).sum(-1)


def setup_inputs():
    s = mx_kscale(K)
    return {"x1": bf(np.random.standard_normal((N, D, H, W)) * 0.5 * s[:D][None, :, None, None]),
            "x2": bf(np.random.standard_normal((N, D, H, W)) * 0.5 * s[D:][None, :, None, None]),
            "c1_w": bf(np.random.standard_normal((O, K)) / np.sqrt(K) / s), "c1_b": bf(np.random.standard_normal(O) * 0.3),
            "c2_w": bf(np.random.standard_normal((O, K)) / np.sqrt(K) / s), "c2_b": bf(np.random.standard_normal(O) * 0.3)}


def reference(x1, x2, c1_w, c1_b, c2_w, c2_b):
    xc = np.concatenate([f64(x1), f64(x2)], axis=1).reshape(N, K, P)
    xq = mxq(xc, 1, "e4m3")
    x1x = (mxq(f64(c1_w), 1, "e4m3") @ xq) + f64(c1_b)[None, :, None]
    x2x = (mxq(f64(c2_w), 1, "e4m3") @ xq) + f64(c2_b)[None, :, None]
    return exp_softmax_pool(x1x), exp_softmax_pool(x2x)

@@ -1,0 +1,386 @@
+from contextlib import ExitStack
+
+import concourse.mybir as mybir
+from concourse.masks import make_identity
+
+F32 = mybir.dt.float32
+BF16 = mybir.dt.bfloat16
+U32 = mybir.dt.uint32
+U8 = mybir.dt.uint8
+FP8X4 = mybir.dt.float8_e4m3fn_x4
+ACT = mybir.ActivationFunctionType
+ALU = mybir.AluOpType
+AX = mybir.AxisListType
+
+P = 128
+PACK = 4
+NB = 4
+POS = 1024
+HALF = 512
+NW = 2
+OT = 4
+NG = NB * NW * OT
+RUN = 4
+VSHARE = 296
+G_FIRST = 5
+G_LAST = 27
+BATCH = 4
+
+
+def is_g(g):
+    return g % 2 == 1 and G_FIRST <= g <= G_LAST
+
+
+FLOPS = 2 * NW * NB * 512 * 1024 * 1024
+
+
+def tile_fr_pa_kernel(tc, x1, x2, c1_w, c1_b, c2_w, c2_b, out_0, out_1):
+    nc = tc.nc
+    xsrc = (x1, x2)
+    with ExitStack() as ctx:
+        keep = ctx.enter_context(tc.tile_pool(name="keep", bufs=1))
+        work = ctx.enter_context(tc.tile_pool(name="work", bufs=3))
+        psum = ctx.enter_context(tc.psum_pool(name="psum", bufs=1))
+        ctx.enter_context(tc.manual_schedule())
+
+        def bank(b, name):
+            return psum.tile([P, HALF], F32, name=name, tag="bank%d" % b)
+
+        ident = keep.tile([P, P], F32, name="ident")
+        make_identity(nc, ident[:])
+        warm_in = keep.tile([P, 1], F32, name="warm_in")
+        warm_out = keep.tile([P, 1], F32, name="warm_out")
+        nc.vector.memset(warm_in[:], 0.0)
+        nc.scalar.activation(out=warm_out[:], in_=warm_in[:], func=ACT.Exp)
+        braw = keep.tile([8, P], BF16, name="braw")
+        bwide = keep.tile([P, P], F32, name="bwide")
+        nc.vector.memset(bwide[:], 0.0)
+        result = keep.tile([P, P], F32, name="result")
+        nc.vector.memset(result[:], 0.0)
+        negm = {}
+        sume = keep.tile([P, NG], F32, name="sume")
+        sd = keep.tile([P, 2, NG], F32, name="sd")
+        nc.vector.memset(sd[:], 0.0)
+        zeros = keep.tile([P, NG], F32, name="zeros")
+        nc.vector.memset(zeros[:], 0.0)
+        ones = keep.tile([P, 1], F32, name="ones")
+        nc.vector.memset(ones[:], 1.0)
+        junk = keep.tile([P, HALF], F32, name="junk")
+        rec = keep.tile([P, NG], F32, name="rec")
+
+        wraw0 = keep.tile([P, 2, 1024], BF16, name="wraw0")
+        wraw1 = keep.tile([P, 2, 1024], BF16, name="wraw1")
+        wraw2 = keep.tile([P, 4, 1024], BF16, name="wraw2")
+        xraw = {}
+
+        def load_x(n, c):
+            t = work.tile([P, PACK, POS], BF16, name="xraw%d%d" % (n, c), tag="xraw", bufs=6)
+            nc.sync.dma_start(out=t[:], in_=xsrc[c][n].rearrange("(p j) h w -> p j (h w)", j=PACK))
+            xraw[(n, c)] = t
+
+        nc.sync.dma_start(out=braw[0:4, :], in_=c1_b.rearrange("(t p) -> t p", p=P))
+        nc.sync.dma_start(out=braw[4:8, :], in_=c2_b.rearrange("(t p) -> t p", p=P))
+        load_x(0, 0)
+        nc.sync.dma_start(out=wraw0[:], in_=c1_w[0:256, :].rearrange("(t p) k -> p t k", p=P))
+        load_x(0, 1)
+        nc.sync.dma_start(out=wraw1[:], in_=c1_w[256:512, :].rearrange("(t p) k -> p t k", p=P))
+        nc.sync.dma_start(out=wraw2[:], in_=c2_w.rearrange("(t p) k -> p t k", p=P))
+        for n in range(1, NB - 1):
+            load_x(n, 0)
+            load_x(n, 1)
+
+        def wrow(j):
+            if j < 2:
+                return wraw0[:, j, :].bitcast(F32)
+            if j < 4:
+                return wraw1[:, j - 2, :].bitcast(F32)
+            return wraw2[:, j - 4, :].bitcast(F32)
+
+        wq = {}
+        ws = {}
+
+        def transpose_w(tiles, banks):
+            turned = []
+            for j, b in zip(tiles, banks):
+                words = wrow(j)
+                wt = bank(b, "wt%d" % j)
+                for c in range(2):
+                    for u in range(2):
+                        q = 2 * c + u
+                        nc.tensor.transpose(
+                            out=wt[:, q * P : (q + 1) * P],
+                            in_=words[:, 256 * c + u : 256 * c + 256 : 2],
+                            identity=ident[:],
+                        )
+                turned.append(wt)
+            return tiles, turned
+
+        def finish_w(prepared):
+            tiles, turned = prepared
+            nt = len(tiles)
+            gw = work.tile([P, nt * 1024], BF16, name="gw%d" % tiles[0], tag="gw", bufs=2, align_bytes=64)
+            codes = keep.tile([P, nt * 256], U32, name="wq%d" % tiles[0], align_bytes=64)
+            plane = keep.tile([P, nt * 256], U8, name="ws%d" % tiles[0], align_bytes=64)
+            for i, j in enumerate(tiles):
+                nc.scalar.copy(
+                    out=gw[:, i * 1024 : (i + 1) * 1024].bitcast(F32).rearrange("p (c o u) -> p c o u", c=2, u=2),
+                    in_=turned[i][:].rearrange("p (c u o) -> p c o u", c=2, u=2),
+                )
+                wq[j] = codes[:, i * 256 : (i + 1) * 256]
+                ws[j] = plane[:, i * 256 : (i + 1) * 256]
+            nc.vector.quantize_mx(out=codes[:].bitcast(FP8X4), scales=plane[:], in_=gw[:])
+
+        bias = keep.tile([P, 8], F32, name="bias")
+
+        def prep_bias():
+            bt = bank(2, "bt")
+            nc.tensor.transpose(out=bt[:, 0:P], in_=bwide[:], identity=ident[:])
+            nc.vector.tensor_copy(out=bias[:], in_=bt[:, 0:8])
+
+        xq = {}
+        xs = {}
+        xg = {}
+
+        def new_x(n):
+            xg[n] = work.tile([P, 2, POS, PACK], BF16, name="xg%d" % n, tag="xg", bufs=2, align_bytes=64)
+            xq[n] = keep.tile([P, 2, POS], U32, name="xq%d" % n, align_bytes=64)
+            xs[n] = keep.tile([P, 2, POS], U8, name="xs%d" % n, align_bytes=64)
+
+        def views(n, c, lo, hi):
+            dst = xg[n][:, c, lo:hi, :].rearrange("p (q i) t -> p q t i", i=RUN)
+            src = xraw[(n, c)][:, :, lo:hi].rearrange("p t (q i) -> p q t i", i=RUN)
+            return dst, src
+
+        def quant_x(n, c, lo, hi):
+            nc.vector.quantize_mx(
+                out=xq[n][:, c, lo:hi].bitcast(FP8X4),
+                scales=xs[n][:, c, lo:hi],
+                in_=xg[n][:, c, lo:hi, :].rearrange("p w t -> p (w t)"),
+            )
+
+        def regroup_head(c):
+            for h in range(2):
+                dst, src = views(0, c, h * HALF, h * HALF + VSHARE)
+                nc.vector.tensor_copy(out=dst, in_=src)
+                dst, src = views(0, c, h * HALF + VSHARE, (h + 1) * HALF)
+                nc.scalar.copy(out=dst, in_=src)
+
+        def regroup_gpsimd(n, c, h):
+            nc.gpsimd.tensor_scalar(
+                out=xg[n][:, c, h * HALF : (h + 1) * HALF, :],
+                in0=xraw[(n, c)][:, :, h * HALF : (h + 1) * HALF].rearrange("p t w -> p w t"),
+                scalar1=1.0,
+                scalar2=0.0,
+                op0=ALU.mult,
+                op1=ALU.add,
+            )
+
+        ybank = {}
+        ysb = {}
+        prod = {}
+        acc = {}
+        atile = {}
+        etile = {}
+
+        def column(g):
+            n, j = divmod(g, 8)
+            return (j // OT) * (NB * OT) + n * OT + j % OT
+
+        def stage_mm(g):
+            n, j = divmod(g, 8)
+            if g < 4:
+                pair = g
+            elif g == NG - 1:
+                pair = 1
+            elif g % 2 == 1 and g >= G_FIRST:
+                pair = 0
+            else:
+                pair = (1, 0, 2, 3)[g % 4]
+            ybank[g] = [bank(2 * pair + h, "y%d_%d" % (g, h)) for h in range(2)]
+            for h in range(2):
+                for c in range(2):
+                    nc.tensor.matmul_mx(
+                        out=ybank[g][h][:],
+                        lhsT=wq[j][:, c * P : (c + 1) * P].bitcast(FP8X4),
+                        lhsT_scale=ws[j][:, c * P : (c + 1) * P],
+                        rhs=xq[n][:, c, h * HALF : (h + 1) * HALF].bitcast(FP8X4),
+                        rhs_scale=xs[n][:, c, h * HALF : (h + 1) * HALF],
+                        start=(c == 0),
+                        stop=(c == 1),
+                    )
+
+        def stage_copy_max(g):
+            ysb[g] = work.tile([P, POS + 2], F32, name="ysb%d" % g, tag="ysb", bufs=4)
+            for h in range(2):
+                nc.vector.tensor_scalar(
+                    out=ysb[g][:, h * HALF : (h + 1) * HALF],
+                    in0=ybank[g][h][:],
+                    scalar1=1.0,
+                    scalar2=None,
+                    op0=ALU.mult,
+                    op1=ALU.max,
+                    accum_out=ysb[g][:, POS + h : POS + h + 1],
+                )
+
+        def stage_a(g):
+            j = g % 8
+            atile[g] = work.tile([P, POS + 2], F32, name="a%d" % g, tag="a")
+            if is_g(g):
+                nc.scalar.activation(out=atile[g][:], in_=ysb[g][:], func=ACT.Exp, bias=bias[:, j : j + 1], scale=1.0)
+                return
+            for h in range(2):
+                nc.scalar.activation(
+                    out=atile[g][:, h * HALF : (h + 1) * HALF],
+                    in_=ybank[g][h][:],
+                    func=ACT.Exp,
+                    bias=bias[:, j : j + 1],
+                    scale=1.0,
+                )
+
+        def stage_b(g):
+            negm[g] = work.tile([P, 1], F32, name="negm%d" % g, tag="negm", bufs=4)
+            src = atile[g][:, POS : POS + 2] if is_g(g) else atile[g][:, 0:POS]
+            nc.vector.tensor_reduce(out=negm[g][:], in_=src, axis=AX.X, op=ALU.max, negate=True)
+
+        def stage_c(g):
+            k = column(g)
+            etile[g] = work.tile([P, POS], F32, name="e%d" % g, tag="e")
+            nc.scalar.activation(
+                out=etile[g][:],
+                in_=atile[g][:, 0:POS],
+                func=ACT.Exp,
+                bias=negm[g][:],
+                scale=1.0,
+                accum_out=sume[:, k : k + 1],
+            )
+
+        def stage_d(g):
+            k = column(g)
+            for h in range(2):
+                nc.vector.scalar_tensor_tensor(
+                    out=junk[:],
+                    in0=ybank[g][h][:],
+                    scalar=1.0,
+                    in1=etile[g][:, h * HALF : (h + 1) * HALF],
+                    op0=ALU.mult,
+                    op1=ALU.mult,
+                    accum_out=sd[:, h, k : k + 1],
+                )
+
+        def stage_prod(g):
+            prod[g] = work.tile([P, POS], F32, name="prod%d" % g, tag="prod")
+            nc.gpsimd.tensor_tensor(out=prod[g][:], in0=etile[g][:], in1=ysb[g][:, 0:POS], op=ALU.mult)
+
+        def slot(g):
+            return ((g - G_FIRST) // 2 + 1) % BATCH
+
+        def stage_fold(g):
+            q = slot(g)
+            if q == 0 or g == G_FIRST:
+                acc[0] = bank(6, "acc%d" % g)
+            for blk in range(POS // P):
+                nc.tensor.matmul(
+                    out=acc[0][:, q * P : (q + 1) * P],
+                    lhsT=prod[g][:, blk * P : (blk + 1) * P],
+                    rhs=ident[:],
+                    is_transpose=True,
+                    start=(blk == 0),
+                    stop=(blk == POS // P - 1),
+                )
+
+        def stage_finish(last):
+            hi = slot(last)
+            lo = max(0, hi - (last - G_FIRST) // 2)
+            accsb = work.tile([P, BATCH * P], F32, name="accsb%d" % last, tag="accsb", bufs=2)
+            nc.vector.tensor_copy(out=accsb[:, lo * P : (hi + 1) * P], in_=acc[0][:, lo * P : (hi + 1) * P])
+            for q in range(lo, hi + 1):
+                k = column(last - 2 * (hi - q))
+                nc.tensor.matmul(
+                    out=fin[:, k : k + 1], lhsT=accsb[:, q * P : (q + 1) * P], rhs=ones[:], start=True, stop=True
+                )
+
+        new_x(0)
+        nc.vector.tensor_copy(out=bwide[0:8, :], in_=braw[:])
+        regroup_head(0)
+        quant_x(0, 0, 0, HALF)
+        quant_x(0, 0, HALF, POS)
+        finish_w(transpose_w([0, 1], [0, 1]))
+        prep_bias()
+        regroup_head(1)
+        quant_x(0, 1, 0, HALF)
+        quant_x(0, 1, HALF, POS)
+        finish_w(transpose_w([2, 3], [4, 5]))
+        stage_mm(0)
+        stage_mm(1)
+        late_w = {2: transpose_w([4, 5], [6, 7])}
+        stage_mm(2)
+        load_x(NB - 1, 0)
+        load_x(NB - 1, 1)
+        new_x(1)
+        for c in range(2):
+            for h in range(2):
+                regroup_gpsimd(1, c, h)
+        pieces = [(n, c, h) for n in range(2, NB) for c in range(2) for h in range(2)]
+
+        fin = None
+        for i in range(NG + 2):
+            if is_g(i + 2) and i + 2 > G_FIRST:
+                stage_copy_max(i + 2)
+            if i >= 2:
+                stage_c(i - 2)
+                if i - 2 == NG - 1:
+                    nc.vector.reciprocal(out=rec[:], in_=sume[:])
+                if is_g(i - 2):
+                    stage_prod(i - 2)
+                else:
+                    stage_d(i - 2)
+            if i == NG - 2:
+                stage_mm(NG - 1)
+            if i in late_w:
+                finish_w(late_w[i])
+            if i == G_FIRST - 2:
+                stage_mm(G_FIRST)
+            if i < NG:
+                stage_a(i)
+                stage_b(i)
+            if i == G_FIRST - 2:
+                stage_copy_max(G_FIRST)
+            if i % 8 in (3, 5) and i // 8 + 1 < NB:
+                quant_x(i // 8 + 1, (i % 8 - 3) // 2, 0, POS)
+            if i % 2 == 0 and 0 <= (i - 4) // 2 < len(pieces):
+                n, c, h = pieces[(i - 4) // 2]
+                if c == 0 and h == 0:
+                    new_x(n)
+                regroup_gpsimd(n, c, h)
+            if i == 2:
+                stage_mm(3)
+                late_w[3] = transpose_w([6, 7], [0, 1])
+            if i == 3:
+                stage_mm(4)
+            if i % 2 == 0 and G_FIRST < i + 3 < NG - 1:
+                stage_mm(i + 3)
+            if 3 <= i < NG - 2 and (i + 2 < G_FIRST or i % 2 == 0):
+                stage_mm(i + 2)
+            if i == G_FIRST + 1:
+                fin = bank(7, "fin")
+                nc.tensor.matmul(out=fin[:, 0:NG], lhsT=ident[:], rhs=zeros[:], start=True, stop=True)
+            if is_g(i - 5) and (slot(i - 5) == BATCH - 1 or i - 5 == G_LAST):
+                stage_finish(i - 5)
+            if is_g(i - 4):
+                stage_fold(i - 4)
+
+        num = keep.tile([P, NG], F32, name="num")
+        nc.vector.tensor_add(out=num[:], in0=sd[:, 0, :], in1=sd[:, 1, :])
+        nc.vector.tensor_add(out=num[:], in0=num[:], in1=fin[:, 0:NG])
+        nc.vector.tensor_mul(out=num[:], in0=num[:], in1=rec[:])
+        nc.vector.tensor_add(
+            out=result[:, 0:NG].rearrange("p (w n t) -> p w n t", w=NW, n=NB),
+            in0=num[:].rearrange("p (w n t) -> p w n t", w=NW, n=NB),
+            in1=bias[:].rearrange("p (w t) -> p w t", w=NW).unsqueeze(2).to_broadcast([P, NW, NB, OT]),
+        )
+        rt = bank(0, "rt")
+        nc.tensor.transpose(out=rt[:, 0:P], in_=result[:], identity=ident[:])
+        rows = keep.tile([P, P], F32, name="rows")
+        nc.vector.tensor_copy(out=rows[:], in_=rt[:, 0:P])
+        nc.sync.dma_start(out=out_0.rearrange("n (t p) -> (n t) p", p=P), in_=rows[0:16, :])
+        nc.sync.dma_start(out=out_1.rearrange("n (t p) -> (n t) p", p=P), in_=rows[16:32, :])

@@ -21,14 +21,64 @@ NW = 2
 OT = 4
 NG = NB * NW * OT
 RUN = 4
-VSHARE = 296
-G_FIRST = 5
-G_LAST = 27
-BATCH = 4
+GB = 0
+GS = 2
+G0 = 4
+HEADP = 4
+G1B = (0, 1)
+QALL = (3, 5, 11, 13, 19, 21)
+LB2 = True
+FOLD2 = 1
+LATE31 = True
+HOLD = False
+C1EARLY = True
+LOADS = {(2, 0): (3, 0), (2, 1): (3, 1)}
+HL = 2
+XGB = 2
+W1FIRST = True
+SPAR = 0
+SX1 = 0
+SX = 0
+W2B = [7, 6]
+W2LATE = False
+GQ = 1024
+GP = 1
+GP1 = 2
+SUMS = 3
+W3B = [7, 6]
+W3V = 0
+W2V = 0
+W1V = 0
+WB = True
+WQ = (1,2)
+WC = (1,2)
+AB = 4
+EVB = 2
+PB = 3
+YB = 7
+EGB = 5
+EVEN = 2
+GSTEPS = range(4, 32, 2)
+QSTEP = (3, 5)
+VSHARE = 256
+LAG = 2
+BATCH = 3
+FOLD = 2
+COPY = 2
+LENT_BANKS = (0, 1)
+OWN_BANKS = (2, 3, 4, 5, 6)
+
+
+LSET = range(1, 30, 2)
+VLENTS = list(LSET)
+SLS = ()
+LENTS = sorted(VLENTS + list(SLS))
+PLAG = 2
+QHEAD = True
 
 
 def is_g(g):
-    return g % 2 == 1 and G_FIRST <= g <= G_LAST
+    return g in VLENTS
 
 
 FLOPS = 2 * NW * NB * 512 * 1024 * 1024
@@ -68,33 +118,45 @@ def tile_fr_pa_kernel(tc, x1, x2, c1_w, c1_b, c2_w, c2_b, out_0, out_1):
         junk = keep.tile([P, HALF], F32, name="junk")
         rec = keep.tile([P, NG], F32, name="rec")
 
-        wraw0 = keep.tile([P, 2, 1024], BF16, name="wraw0")
-        wraw1 = keep.tile([P, 2, 1024], BF16, name="wraw1")
-        wraw2 = keep.tile([P, 4, 1024], BF16, name="wraw2")
         xraw = {}
+        wraw = {}
+
+        def big(name):
+            return work.tile([P, PACK, POS], BF16, name=name, tag="raw", bufs=5)
 
         def load_x(n, c):
-            t = work.tile([P, PACK, POS], BF16, name="xraw%d%d" % (n, c), tag="xraw", bufs=6)
-            nc.sync.dma_start(out=t[:], in_=xsrc[c][n].rearrange("(p j) h w -> p j (h w)", j=PACK))
-            xraw[(n, c)] = t
+            xraw[(n, c)] = big("xraw%d%d" % (n, c))
+            nc.sync.dma_start(out=xraw[(n, c)][:], in_=xsrc[c][n].rearrange("(p j) h w -> p j (h w)", j=PACK))
 
+        def xhalf(n, c, h):
+            return xraw[(n, c)][:].rearrange("p t w -> p (t w)")[:, h * PACK * HALF : (h + 1) * PACK * HALF].rearrange("p (t w) -> p t w", t=PACK)
+
+        def load_x_half(n, c, h):
+            if h == 0:
+                xraw[(n, c)] = big("xraw%d%d" % (n, c))
+            nc.sync.dma_start(
+                out=xhalf(n, c, h),
+                in_=xsrc[c][n].rearrange("(p j) h w -> p j (h w)", j=PACK)[:, :, h * HALF : (h + 1) * HALF],
+            )
+
+        def load_w(w, lo, hi):
+            if lo == 0:
+                wraw[w] = big("wraw%d" % w)
+            src = (c1_w, c2_w)[w][lo * P : hi * P, :].rearrange("(t p) k -> p t k", p=P)
+            nc.sync.dma_start(out=wraw[w][:, lo:hi, :], in_=src)
+
+        load_w(0, 0, 2)
         nc.sync.dma_start(out=braw[0:4, :], in_=c1_b.rearrange("(t p) -> t p", p=P))
         nc.sync.dma_start(out=braw[4:8, :], in_=c2_b.rearrange("(t p) -> t p", p=P))
-        load_x(0, 0)
-        nc.sync.dma_start(out=wraw0[:], in_=c1_w[0:256, :].rearrange("(t p) k -> p t k", p=P))
-        load_x(0, 1)
-        nc.sync.dma_start(out=wraw1[:], in_=c1_w[256:512, :].rearrange("(t p) k -> p t k", p=P))
-        nc.sync.dma_start(out=wraw2[:], in_=c2_w.rearrange("(t p) k -> p t k", p=P))
-        for n in range(1, NB - 1):
-            load_x(n, 0)
-            load_x(n, 1)
+        for c in range(2):
+            for h in range(2):
+                load_x_half(0, c, h)
+        load_w(0, 2, 4)
+        load_w(1, 0, 4)
+        load_x(1, 0)
 
         def wrow(j):
-            if j < 2:
-                return wraw0[:, j, :].bitcast(F32)
-            if j < 4:
-                return wraw1[:, j - 2, :].bitcast(F32)
-            return wraw2[:, j - 4, :].bitcast(F32)
+            return wraw[j // OT][:, j % OT, :].bitcast(F32)
 
         wq = {}
         ws = {}
@@ -115,20 +177,26 @@ def tile_fr_pa_kernel(tc, x1, x2, c1_w, c1_b, c2_w, c2_b, out_0, out_1):
                 turned.append(wt)
             return tiles, turned
 
-        def finish_w(prepared):
+        gw = {}
+
+        def copy_w(prepared, nv=0):
             tiles, turned = prepared
             nt = len(tiles)
-            gw = work.tile([P, nt * 1024], BF16, name="gw%d" % tiles[0], tag="gw", bufs=2, align_bytes=64)
+            gw[tiles[0]] = work.tile([P, nt * 1024], BF16, name="gw%d" % tiles[0], tag="gw", bufs=2, align_bytes=64)
+            for i, j in enumerate(tiles):
+                (nc.vector.tensor_copy if i < nv else nc.scalar.copy)(
+                    out=gw[tiles[0]][:, i * 1024 : (i + 1) * 1024].bitcast(F32).rearrange("p (c o u) -> p c o u", c=2, u=2),
+                    in_=turned[i][:].rearrange("p (c u o) -> p c o u", c=2, u=2),
+                )
+
+        def quant_w(tiles):
+            nt = len(tiles)
             codes = keep.tile([P, nt * 256], U32, name="wq%d" % tiles[0], align_bytes=64)
             plane = keep.tile([P, nt * 256], U8, name="ws%d" % tiles[0], align_bytes=64)
             for i, j in enumerate(tiles):
-                nc.scalar.copy(
-                    out=gw[:, i * 1024 : (i + 1) * 1024].bitcast(F32).rearrange("p (c o u) -> p c o u", c=2, u=2),
-                    in_=turned[i][:].rearrange("p (c u o) -> p c o u", c=2, u=2),
-                )
                 wq[j] = codes[:, i * 256 : (i + 1) * 256]
                 ws[j] = plane[:, i * 256 : (i + 1) * 256]
-            nc.vector.quantize_mx(out=codes[:].bitcast(FP8X4), scales=plane[:], in_=gw[:])
+            nc.vector.quantize_mx(out=codes[:].bitcast(FP8X4), scales=plane[:], in_=gw[tiles[0]][:])
 
         bias = keep.tile([P, 8], F32, name="bias")
 
@@ -141,66 +209,84 @@ def tile_fr_pa_kernel(tc, x1, x2, c1_w, c1_b, c2_w, c2_b, out_0, out_1):
         xs = {}
         xg = {}
 
-        def new_x(n):
-            xg[n] = work.tile([P, 2, POS, PACK], BF16, name="xg%d" % n, tag="xg", bufs=2, align_bytes=64)
-            xq[n] = keep.tile([P, 2, POS], U32, name="xq%d" % n, align_bytes=64)
-            xs[n] = keep.tile([P, 2, POS], U8, name="xs%d" % n, align_bytes=64)
+        def new_x(n, c):
+            xg[(n, c)] = work.tile(
+                [P, POS, PACK], BF16, name="xg%d%d" % (n, c), tag="xg" if n == 0 else "xh", bufs=2 if n == 0 else XGB, align_bytes=64
+            )
+            if c == 0:
+                xq[n] = keep.tile([P, 2, POS], U32, name="xq%d" % n, align_bytes=64)
+                xs[n] = keep.tile([P, 2, POS], U8, name="xs%d" % n, align_bytes=64)
 
         def views(n, c, lo, hi):
-            dst = xg[n][:, c, lo:hi, :].rearrange("p (q i) t -> p q t i", i=RUN)
-            src = xraw[(n, c)][:, :, lo:hi].rearrange("p t (q i) -> p q t i", i=RUN)
+            dst = xg[(n, c)][:, lo:hi, :].rearrange("p (q i) t -> p q t i", i=RUN)
+            src = xhalf(n, c, lo // HALF)[:, :, lo % HALF : (hi - 1) % HALF + 1].rearrange("p t (q i) -> p q t i", i=RUN)
             return dst, src
 
+        ready = {}
+
         def quant_x(n, c, lo, hi):
+            assert n == 0 or ready[(n, c)] == 2048 * 1, (n, c, ready)
             nc.vector.quantize_mx(
                 out=xq[n][:, c, lo:hi].bitcast(FP8X4),
                 scales=xs[n][:, c, lo:hi],
-                in_=xg[n][:, c, lo:hi, :].rearrange("p w t -> p (w t)"),
+                in_=xg[(n, c)][:, lo:hi, :].rearrange("p w t -> p (w t)"),
             )
 
-        def regroup_head(c):
-            for h in range(2):
-                dst, src = views(0, c, h * HALF, h * HALF + VSHARE)
-                nc.vector.tensor_copy(out=dst, in_=src)
-                dst, src = views(0, c, h * HALF + VSHARE, (h + 1) * HALF)
-                nc.scalar.copy(out=dst, in_=src)
+        def regroup_v(c, h):
+            dst, src = views(0, c, h * HALF, h * HALF + VSHARE)
+            nc.vector.tensor_copy(out=dst, in_=src)
+
+        def regroup_s(c, h):
+            dst, src = views(0, c, h * HALF + VSHARE, (h + 1) * HALF)
+            nc.scalar.copy(out=dst, in_=src)
 
         def regroup_gpsimd(n, c, h):
-            nc.gpsimd.tensor_scalar(
-                out=xg[n][:, c, h * HALF : (h + 1) * HALF, :],
-                in0=xraw[(n, c)][:, :, h * HALF : (h + 1) * HALF].rearrange("p t w -> p w t"),
-                scalar1=1.0,
-                scalar2=0.0,
-                op0=ALU.mult,
-                op1=ALU.add,
-            )
+            end = (h + 1) * HALF - (SX1 if n == 1 else SX)
+            ready[(n, c)] = ready.get((n, c), 0) + 2 * (end - h * HALF)
+            gp = (end - h * HALF) // (GP1 if n == 1 else GP)
+            for lo in range(h * HALF, end, gp):
+                nc.gpsimd.tensor_scalar(
+                    out=xg[(n, c)][:, lo : lo + gp, :],
+                    in0=xraw[(n, c)][:, :, lo : lo + gp].rearrange("p t w -> p w t"),
+                    scalar1=1.0,
+                    scalar2=0.0,
+                    op0=ALU.mult,
+                    op1=ALU.add,
+                )
+
+        def regroup_sx(n, c, h):
+            sx = SX1 if n == 1 else SX
+            if sx == 0:
+                return
+            lo, hi = (h + 1) * HALF - sx, (h + 1) * HALF
+            ready[(n, c)] = ready.get((n, c), 0) + 2 * sx
+            dst = xg[(n, c)][:, lo:hi, :].rearrange("p (q i) t -> p q t i", i=RUN)
+            src = xraw[(n, c)][:, :, lo:hi].rearrange("p t (q i) -> p q t i", i=RUN)
+            nc.scalar.copy(out=dst, in_=src)
 
         ybank = {}
         ysb = {}
         prod = {}
-        acc = {}
         atile = {}
         etile = {}
+        turn = [0]
 
         def column(g):
             n, j = divmod(g, 8)
             return (j // OT) * (NB * OT) + n * OT + j % OT
 
-        def stage_mm(g):
+        def stage_mm(g, halves=(0, 1)):
             n, j = divmod(g, 8)
-            if g < 4:
-                pair = g
-            elif g == NG - 1:
-                pair = 1
-            elif g % 2 == 1 and g >= G_FIRST:
-                pair = 0
-            else:
-                pair = (1, 0, 2, 3)[g % 4]
-            ybank[g] = [bank(2 * pair + h, "y%d_%d" % (g, h)) for h in range(2)]
-            for h in range(2):
+            for h in halves:
+                if is_g(g):
+                    b = G1B[h] if g == 1 else LENT_BANKS[h]
+                else:
+                    b = OWN_BANKS[turn[0] % len(OWN_BANKS)]
+                    turn[0] += 1
+                ybank[(g, h)] = bank(b, "y%d_%d" % (g, h))
                 for c in range(2):
                     nc.tensor.matmul_mx(
-                        out=ybank[g][h][:],
+                        out=ybank[(g, h)][:],
                         lhsT=wq[j][:, c * P : (c + 1) * P].bitcast(FP8X4),
                         lhsT_scale=ws[j][:, c * P : (c + 1) * P],
                         rhs=xq[n][:, c, h * HALF : (h + 1) * HALF].bitcast(FP8X4),
@@ -209,12 +295,13 @@ def tile_fr_pa_kernel(tc, x1, x2, c1_w, c1_b, c2_w, c2_b, out_0, out_1):
                         stop=(c == 1),
                     )
 
-        def stage_copy_max(g):
-            ysb[g] = work.tile([P, POS + 2], F32, name="ysb%d" % g, tag="ysb", bufs=4)
-            for h in range(2):
+        def stage_copy_max(g, halves=(0, 1)):
+            if 0 in halves:
+                ysb[g] = work.tile([P, POS + 2], F32, name="ysb%d" % g, tag="ysb", bufs=YB)
+            for h in halves:
                 nc.vector.tensor_scalar(
                     out=ysb[g][:, h * HALF : (h + 1) * HALF],
-                    in0=ybank[g][h][:],
+                    in0=ybank[(g, h)][:],
                     scalar1=1.0,
                     scalar2=None,
                     op0=ALU.mult,
@@ -222,29 +309,38 @@ def tile_fr_pa_kernel(tc, x1, x2, c1_w, c1_b, c2_w, c2_b, out_0, out_1):
                     accum_out=ysb[g][:, POS + h : POS + h + 1],
                 )
 
-        def stage_a(g):
+        def stage_a(g, halves=(0, 1)):
             j = g % 8
-            atile[g] = work.tile([P, POS + 2], F32, name="a%d" % g, tag="a")
+            if g not in atile:
+                atile[g] = work.tile([P, POS + 2], F32, name="a%d" % g, tag="a", bufs=AB)
             if is_g(g):
                 nc.scalar.activation(out=atile[g][:], in_=ysb[g][:], func=ACT.Exp, bias=bias[:, j : j + 1], scale=1.0)
                 return
-            for h in range(2):
+            for h in halves:
                 nc.scalar.activation(
                     out=atile[g][:, h * HALF : (h + 1) * HALF],
-                    in_=ybank[g][h][:],
+                    in_=ybank[(g, h)][:],
                     func=ACT.Exp,
                     bias=bias[:, j : j + 1],
                     scale=1.0,
                 )
 
+        def stage_scopy(g):
+            ysb[g] = work.tile([P, POS + 2], F32, name="ysb%d" % g, tag="ysb", bufs=YB)
+            for h in range(2):
+                nc.scalar.copy(out=ysb[g][:, h * HALF : (h + 1) * HALF], in_=ybank[(g, h)][:])
+
         def stage_b(g):
-            negm[g] = work.tile([P, 1], F32, name="negm%d" % g, tag="negm", bufs=4)
+            negm[g] = work.tile([P, 1], F32, name="negm%d" % g, tag="negm", bufs=6)
             src = atile[g][:, POS : POS + 2] if is_g(g) else atile[g][:, 0:POS]
             nc.vector.tensor_reduce(out=negm[g][:], in_=src, axis=AX.X, op=ALU.max, negate=True)
 
         def stage_c(g):
             k = column(g)
-            etile[g] = work.tile([P, POS], F32, name="e%d" % g, tag="e")
+            if g in LENTS:
+                etile[g] = work.tile([P, POS], F32, name="e%d" % g, tag="eg", bufs=EGB)
+            else:
+                etile[g] = work.tile([P, POS], F32, name="e%d" % g, tag="ev", bufs=EVB)
             nc.scalar.activation(
                 out=etile[g][:],
                 in_=atile[g][:, 0:POS],
@@ -254,12 +350,12 @@ def tile_fr_pa_kernel(tc, x1, x2, c1_w, c1_b, c2_w, c2_b, out_0, out_1):
                 accum_out=sume[:, k : k + 1],
             )
 
-        def stage_d(g):
+        def stage_d(g, halves=(0, 1)):
             k = column(g)
-            for h in range(2):
+            for h in halves:
                 nc.vector.scalar_tensor_tensor(
                     out=junk[:],
-                    in0=ybank[g][h][:],
+                    in0=ybank[(g, h)][:],
                     scalar=1.0,
                     in1=etile[g][:, h * HALF : (h + 1) * HALF],
                     op0=ALU.mult,
@@ -268,19 +364,20 @@ def tile_fr_pa_kernel(tc, x1, x2, c1_w, c1_b, c2_w, c2_b, out_0, out_1):
                 )
 
         def stage_prod(g):
-            prod[g] = work.tile([P, POS], F32, name="prod%d" % g, tag="prod")
-            nc.gpsimd.tensor_tensor(out=prod[g][:], in0=etile[g][:], in1=ysb[g][:, 0:POS], op=ALU.mult)
+            prod[g] = work.tile([P, POS], F32, name="prod%d" % g, tag="prod", bufs=PB)
+            for lo in range(0, POS, GQ):
+                nc.gpsimd.tensor_tensor(
+                    out=prod[g][:, lo : lo + GQ], in0=etile[g][:, lo : lo + GQ], in1=ysb[g][:, lo : lo + GQ], op=ALU.mult
+                )
 
         def slot(g):
-            return ((g - G_FIRST) // 2 + 1) % BATCH
+            return (LENTS.index(g) - len(LENTS) + 1) % BATCH
 
         def stage_fold(g):
             q = slot(g)
-            if q == 0 or g == G_FIRST:
-                acc[0] = bank(6, "acc%d" % g)
             for blk in range(POS // P):
                 nc.tensor.matmul(
-                    out=acc[0][:, q * P : (q + 1) * P],
+                    out=sums[:, q * P : (q + 1) * P],
                     lhsT=prod[g][:, blk * P : (blk + 1) * P],
                     rhs=ident[:],
                     is_transpose=True,
@@ -290,94 +387,186 @@ def tile_fr_pa_kernel(tc, x1, x2, c1_w, c1_b, c2_w, c2_b, out_0, out_1):
 
         def stage_finish(last):
             hi = slot(last)
-            lo = max(0, hi - (last - G_FIRST) // 2)
+            lo = max(0, hi - LENTS.index(last))
             accsb = work.tile([P, BATCH * P], F32, name="accsb%d" % last, tag="accsb", bufs=2)
-            nc.vector.tensor_copy(out=accsb[:, lo * P : (hi + 1) * P], in_=acc[0][:, lo * P : (hi + 1) * P])
+            nc.vector.tensor_copy(out=accsb[:, lo * P : (hi + 1) * P], in_=sums[:, lo * P : (hi + 1) * P])
             for q in range(lo, hi + 1):
-                k = column(last - 2 * (hi - q))
+                k = column(LENTS[LENTS.index(last) - (hi - q)])
                 nc.tensor.matmul(
                     out=fin[:, k : k + 1], lhsT=accsb[:, q * P : (q + 1) * P], rhs=ones[:], start=True, stop=True
                 )
 
-        new_x(0)
+        new_x(0, 0)
+        new_x(0, 1)
         nc.vector.tensor_copy(out=bwide[0:8, :], in_=braw[:])
-        regroup_head(0)
-        quant_x(0, 0, 0, HALF)
-        quant_x(0, 0, HALF, POS)
-        finish_w(transpose_w([0, 1], [0, 1]))
+        w0 = transpose_w([0, 1], [0, 1])
+        copy_w(w0)
+        regroup_v(0, 0)
+        regroup_s(0, 0)
+        quant_w([0, 1])
         prep_bias()
-        regroup_head(1)
+        regroup_v(0, 1)
+        regroup_s(0, 1)
+        quant_x(0, 0, 0, HALF)
+        regroup_v(1, 0)
+        regroup_s(1, 0)
+        quant_x(0, 0, HALF, POS)
+        regroup_v(1, 1)
         quant_x(0, 1, 0, HALF)
+        w1 = transpose_w([2, 3], [6, 7])
+        stage_mm(0, (0,))
+        regroup_s(1, 1)
+        if W1FIRST:
+            copy_w(w1, W1V)
+        stage_a(0, (0,))
         quant_x(0, 1, HALF, POS)
-        finish_w(transpose_w([2, 3], [4, 5]))
-        stage_mm(0)
+        stage_mm(0, (1,))
         stage_mm(1)
-        late_w = {2: transpose_w([4, 5], [6, 7])}
-        stage_mm(2)
-        load_x(NB - 1, 0)
-        load_x(NB - 1, 1)
-        new_x(1)
-        for c in range(2):
-            for h in range(2):
-                regroup_gpsimd(1, c, h)
-        pieces = [(n, c, h) for n in range(2, NB) for c in range(2) for h in range(2)]
+        if W1FIRST:
+            quant_w([2, 3])
+        stage_copy_max(1)
+        stage_a(0, (1,))
+        if not W1FIRST:
+            copy_w(w1, W1V)
+        stage_b(0)
+        if not W1FIRST:
+            quant_w([2, 3])
+        load_x(1, 1)
+        spieces = []
+        order = [(n, c) for n in range(1, NB) for c in range(2)]
+        qstep = {(n, c): QALL[2 * (n - 1) + c] for n, c in order}
 
-        fin = None
-        for i in range(NG + 2):
-            if is_g(i + 2) and i + 2 > G_FIRST:
-                stage_copy_max(i + 2)
-            if i >= 2:
-                stage_c(i - 2)
-                if i - 2 == NG - 1:
+        def piece(n, c, h):
+            if h == 0:
+                new_x(n, c)
+            regroup_gpsimd(n, c, h)
+            spieces.append((n, c, h))
+
+        waiting = []
+        held = [False]
+
+        def after_quant(n, c):
+            held[0] = False
+            return
+
+        pieces = [(n, c, h) for n, c in order for h in range(2)]
+        for k in range(HEADP):
+            piece(*pieces[k])
+        load_x(2, 0)
+        load_x(2, 1)
+        issued = [HEADP]
+        if W2LATE:
+            stage_mm(2)
+        w2 = transpose_w([4, 5], W2B)
+        if not W2LATE:
+            stage_mm(2)
+        sums = None
+
+
+        def quants(i):
+            for n, c in order:
+                if i == qstep[(n, c)]:
+                    while spieces and spieces[0][:2] == (n, c) and (SX1 if n == 1 else SX):
+                        regroup_sx(*spieces.pop(0))
+                    quant_x(n, c, 0, POS)
+                    after_quant(n, c)
+
+        done = []
+        folded = []
+        for i in range(NG + LAG):
+            while spieces and (SX if spieces[0][0] > 1 else SX1) == 0:
+                spieces.pop(0)
+            if spieces and (i % 2 == SPAR or spieces[0][0] == 1):
+                regroup_sx(*spieces.pop(0))
+            if QHEAD:
+                quants(i)
+            if is_g(i + COPY) and i + COPY > 1:
+                stage_copy_max(i + COPY, (0,))
+                if not LB2:
+                    stage_mm(i + COPY, (1,))
+                if C1EARLY:
+                    stage_copy_max(i + COPY, (1,))
+            if i >= LAG:
+                stage_c(i - LAG)
+                if i - LAG == NG - 1:
                     nc.vector.reciprocal(out=rec[:], in_=sume[:])
-                if is_g(i - 2):
-                    stage_prod(i - 2)
-                else:
-                    stage_d(i - 2)
-            if i == NG - 2:
+                if (i - LAG) not in LENTS and i - LAG < NG - 1:
+                    stage_d(i - LAG)
+            for g in LENTS:
+                if g + (PLAG if g < 24 else LAG) == i:
+                    waiting.append(g)
+            if LATE31 and i == NG - 4 + LAG:
                 stage_mm(NG - 1)
-            if i in late_w:
-                finish_w(late_w[i])
-            if i == G_FIRST - 2:
-                stage_mm(G_FIRST)
+            if not held[0]:
+                while waiting:
+                    stage_prod(waiting.pop(0))
             if i < NG:
-                stage_a(i)
-                stage_b(i)
-            if i == G_FIRST - 2:
-                stage_copy_max(G_FIRST)
-            if i % 8 in (3, 5) and i // 8 + 1 < NB:
-                quant_x(i // 8 + 1, (i % 8 - 3) // 2, 0, POS)
-            if i % 2 == 0 and 0 <= (i - 4) // 2 < len(pieces):
-                n, c, h = pieces[(i - 4) // 2]
-                if c == 0 and h == 0:
-                    new_x(n)
-                regroup_gpsimd(n, c, h)
-            if i == 2:
-                stage_mm(3)
-                late_w[3] = transpose_w([6, 7], [0, 1])
-            if i == 3:
-                stage_mm(4)
-            if i % 2 == 0 and G_FIRST < i + 3 < NG - 1:
-                stage_mm(i + 3)
-            if 3 <= i < NG - 2 and (i + 2 < G_FIRST or i % 2 == 0):
-                stage_mm(i + 2)
-            if i == G_FIRST + 1:
-                fin = bank(7, "fin")
-                nc.tensor.matmul(out=fin[:, 0:NG], lhsT=ident[:], rhs=zeros[:], start=True, stop=True)
-            if is_g(i - 5) and (slot(i - 5) == BATCH - 1 or i - 5 == G_LAST):
-                stage_finish(i - 5)
-            if is_g(i - 4):
-                stage_fold(i - 4)
+                if i > 0:
+                    stage_a(i)
+                if i in SLS:
+                    stage_scopy(i)
+                if i == WC[0]:
+                    copy_w(w2, W2V)
+                    w3 = transpose_w([6, 7], W3B)
+                if i == WC[1]:
+                    copy_w(w3, W3V)
+                if i == WQ[0] and not WB:
+                    quant_w([4, 5])
+                if i == WQ[1] and not WB:
+                    quant_w([6, 7])
+                if i > 0:
+                    stage_b(i)
+                if i == WQ[0] and WB:
+                    quant_w([4, 5])
+                if i == WQ[1] and WB:
+                    quant_w([6, 7])
+            if is_g(i + COPY) and i + COPY > 1 and not C1EARLY:
+                stage_copy_max(i + COPY, (1,))
+            if not QHEAD:
+                quants(i)
+            while issued[0] < len(pieces) and G0 + GS * (issued[0] - HEADP) + GB * ((issued[0] - HEADP) // 4) <= i:
+                n, c, h = pieces[issued[0]]
+                piece(n, c, h)
+                issued[0] += 1
+                if h == 1 and (n, c) in LOADS:
+                    load_x(*LOADS[(n, c)])
+            if i == SUMS:
+                sums = bank(7, "sums")
+                fin = sums[:, BATCH * P : BATCH * P + NG]
+                nc.tensor.matmul(out=fin, lhsT=ident[:], rhs=zeros[:], start=True, stop=True)
+            if is_g(i + COPY + 1) and i + COPY + 1 > 1:
+                stage_mm(i + COPY + 1, (0, 1) if LB2 else (0,))
+            if 2 < i + EVEN < NG - (1 if LATE31 else 0) and not is_g(i + EVEN):
+                stage_mm(i + EVEN)
+            for g in LENTS:
+                if g in folded and g not in done and slot(g) == BATCH - 1 and g != LENTS[-1]:
+                    stage_finish(g)
+                    done.append(g)
+            for g in LENTS:
+                if g + (PLAG + FOLD if g < 24 else LAG + FOLD2) <= i and g not in folded and g in prod and i < NG + LAG:
+                    stage_fold(g)
+                    folded.append(g)
+        for g in LENTS:
+            if g not in folded:
+                if g not in prod:
+                    stage_prod(g)
+                stage_fold(g)
+            if (slot(g) == BATCH - 1 or g == LENTS[-1]) and g not in done:
+                stage_finish(g)
+        part = keep.tile([P, NG], F32, name="part")
+        stage_d(NG - 1, (0,))
+        nc.vector.tensor_add(out=part[:], in0=sd[:, 0, :], in1=fin)
+        stage_d(NG - 1, (1,))
 
+        nc.vector.tensor_mul(out=part[:], in0=part[:], in1=rec[:])
         num = keep.tile([P, NG], F32, name="num")
-        nc.vector.tensor_add(out=num[:], in0=sd[:, 0, :], in1=sd[:, 1, :])
-        nc.vector.tensor_add(out=num[:], in0=num[:], in1=fin[:, 0:NG])
-        nc.vector.tensor_mul(out=num[:], in0=num[:], in1=rec[:])
+        nc.vector.tensor_mul(out=num[:], in0=sd[:, 1, :], in1=rec[:])
         nc.vector.tensor_add(
-            out=result[:, 0:NG].rearrange("p (w n t) -> p w n t", w=NW, n=NB),
-            in0=num[:].rearrange("p (w n t) -> p w n t", w=NW, n=NB),
+            out=part[:].rearrange("p (w n t) -> p w n t", w=NW, n=NB),
+            in0=part[:].rearrange("p (w n t) -> p w n t", w=NW, n=NB),
             in1=bias[:].rearrange("p (w t) -> p w t", w=NW).unsqueeze(2).to_broadcast([P, NW, NB, OT]),
         )
+        nc.vector.tensor_add(out=result[:, 0:NG], in0=num[:], in1=part[:])
         rt = bank(0, "rt")
         nc.tensor.transpose(out=rt[:, 0:P], in_=result[:], identity=ident[:])
         rows = keep.tile([P, P], F32, name="rows")

@@ -21,29 +21,41 @@ NW = 2
 OT = 4
 NG = NB * NW * OT
 RUN = 4
+FENCE = True
+QUOTA = 1
+H1NOW = False
+GUARD = True
+LASTFOLD = 33
+KEEPHEAD = True
+FB = 7
+PVB = 2
+XFIRST = False
+SPLITC = True
+FIN = 1
+FINS = False
 GB = 0
 GS = 2
 G0 = 4
 HEADP = 4
 G1B = (0, 1)
-QALL = (3, 5, 11, 13, 19, 21)
+QALL = (1, 4, 8, 12, 16, 20)
 LB2 = True
 FOLD2 = 1
 LATE31 = True
-HOLD = False
+HOLD = True
 C1EARLY = True
-LOADS = {(2, 0): (3, 0), (2, 1): (3, 1)}
-HL = 2
-XGB = 2
+LOADS = {(1, 1): (2, 1), (2, 0): (3, 0), (2, 1): (3, 1)}
+HL = 1
+XGB = 1
 W1FIRST = True
 SPAR = 0
 SX1 = 0
 SX = 0
-W2B = [7, 6]
+W2B = [6, 7]
 W2LATE = False
 GQ = 1024
 GP = 1
-GP1 = 2
+GP1 = 1
 SUMS = 3
 W3B = [7, 6]
 W3V = 0
@@ -54,13 +66,13 @@ WQ = (1,2)
 WC = (1,2)
 AB = 4
 EVB = 2
-PB = 3
-YB = 7
-EGB = 5
+PB = 4
+YB = 8
+EGB = 8
 EVEN = 2
 GSTEPS = range(4, 32, 2)
 QSTEP = (3, 5)
-VSHARE = 256
+VSHARE = 296
 LAG = 2
 BATCH = 3
 FOLD = 2
@@ -72,9 +84,10 @@ OWN_BANKS = (2, 3, 4, 5, 6)
 LSET = range(1, 30, 2)
 VLENTS = list(LSET)
 SLS = ()
-LENTS = sorted(VLENTS + list(SLS))
+PLS = ()
+LENTS = sorted(VLENTS + list(SLS) + list(PLS))
 PLAG = 2
-QHEAD = True
+QHEAD = False
 
 
 def is_g(g):
@@ -115,6 +128,7 @@ def tile_fr_pa_kernel(tc, x1, x2, c1_w, c1_b, c2_w, c2_b, out_0, out_1):
         nc.vector.memset(zeros[:], 0.0)
         ones = keep.tile([P, 1], F32, name="ones")
         nc.vector.memset(ones[:], 1.0)
+        sumlast = keep.tile([P, 1], F32, name="sumlast")
         junk = keep.tile([P, HALF], F32, name="junk")
         rec = keep.tile([P, NG], F32, name="rec")
 
@@ -145,12 +159,15 @@ def tile_fr_pa_kernel(tc, x1, x2, c1_w, c1_b, c2_w, c2_b, out_0, out_1):
             src = (c1_w, c2_w)[w][lo * P : hi * P, :].rearrange("(t p) k -> p t k", p=P)
             nc.sync.dma_start(out=wraw[w][:, lo:hi, :], in_=src)
 
+        if XFIRST:
+            load_x_half(0, 0, 0)
         load_w(0, 0, 2)
         nc.sync.dma_start(out=braw[0:4, :], in_=c1_b.rearrange("(t p) -> t p", p=P))
         nc.sync.dma_start(out=braw[4:8, :], in_=c2_b.rearrange("(t p) -> t p", p=P))
         for c in range(2):
             for h in range(2):
-                load_x_half(0, c, h)
+                if not XFIRST or c + h > 0:
+                    load_x_half(0, c, h)
         load_w(0, 2, 4)
         load_w(1, 0, 4)
         load_x(1, 0)
@@ -278,7 +295,7 @@ def tile_fr_pa_kernel(tc, x1, x2, c1_w, c1_b, c2_w, c2_b, out_0, out_1):
         def stage_mm(g, halves=(0, 1)):
             n, j = divmod(g, 8)
             for h in halves:
-                if is_g(g):
+                if is_g(g) or (LB2 and g == 29):
                     b = G1B[h] if g == 1 else LENT_BANKS[h]
                 else:
                     b = OWN_BANKS[turn[0] % len(OWN_BANKS)]
@@ -337,18 +354,19 @@ def tile_fr_pa_kernel(tc, x1, x2, c1_w, c1_b, c2_w, c2_b, out_0, out_1):
 
         def stage_c(g):
             k = column(g)
-            if g in LENTS:
+            if g in LENTS and g not in PLS:
                 etile[g] = work.tile([P, POS], F32, name="e%d" % g, tag="eg", bufs=EGB)
             else:
                 etile[g] = work.tile([P, POS], F32, name="e%d" % g, tag="ev", bufs=EVB)
-            nc.scalar.activation(
-                out=etile[g][:],
-                in_=atile[g][:, 0:POS],
-                func=ACT.Exp,
-                bias=negm[g][:],
-                scale=1.0,
-                accum_out=sume[:, k : k + 1],
-            )
+            for h, (lo, hi) in enumerate(((0, HALF), (HALF, POS)) if g == NG - 1 and SPLITC else ((0, POS),)):
+                nc.scalar.activation(
+                    out=etile[g][:, lo:hi],
+                    in_=atile[g][:, lo:hi],
+                    func=ACT.Exp,
+                    bias=negm[g][:],
+                    scale=1.0,
+                    accum_out=sume[:, k : k + 1] if h == 0 else sumlast[:],
+                )
 
         def stage_d(g, halves=(0, 1)):
             k = column(g)
@@ -363,8 +381,25 @@ def tile_fr_pa_kernel(tc, x1, x2, c1_w, c1_b, c2_w, c2_b, out_0, out_1):
                     accum_out=sd[:, h, k : k + 1],
                 )
 
+        fence = [False]
+
         def stage_prod(g):
-            prod[g] = work.tile([P, POS], F32, name="prod%d" % g, tag="prod", bufs=PB)
+            if fence[0]:
+                prod[g] = work.tile([P, POS], F32, name="prod%d" % g, tag="xh", bufs=XGB, align_bytes=64)
+                fence[0] = False
+            else:
+                prod[g] = work.tile(
+                    [P, POS], F32, name="prod%d" % g, tag="prodv" if g in PLS else "prod", bufs=PVB if g in PLS else PB
+                )
+            if g in PLS:
+                for h in range(2):
+                    nc.vector.tensor_tensor(
+                        out=prod[g][:, h * HALF : (h + 1) * HALF],
+                        in0=ybank[(g, h)][:],
+                        in1=etile[g][:, h * HALF : (h + 1) * HALF],
+                        op=ALU.mult,
+                    )
+                return
             for lo in range(0, POS, GQ):
                 nc.gpsimd.tensor_tensor(
                     out=prod[g][:, lo : lo + GQ], in0=etile[g][:, lo : lo + GQ], in1=ysb[g][:, lo : lo + GQ], op=ALU.mult
@@ -373,8 +408,12 @@ def tile_fr_pa_kernel(tc, x1, x2, c1_w, c1_b, c2_w, c2_b, out_0, out_1):
         def slot(g):
             return (LENTS.index(g) - len(LENTS) + 1) % BATCH
 
+        busy = {}
+
         def stage_fold(g):
             q = slot(g)
+            assert q not in busy and (q == 0 or LENTS[LENTS.index(g) - 1] in busy.values() or g == LENTS[0]), (g, busy)
+            busy[q] = g
             for blk in range(POS // P):
                 nc.tensor.matmul(
                     out=sums[:, q * P : (q + 1) * P],
@@ -388,8 +427,12 @@ def tile_fr_pa_kernel(tc, x1, x2, c1_w, c1_b, c2_w, c2_b, out_0, out_1):
         def stage_finish(last):
             hi = slot(last)
             lo = max(0, hi - LENTS.index(last))
+            assert [busy[q] for q in range(lo, hi + 1)] == LENTS[LENTS.index(last) - (hi - lo) : LENTS.index(last) + 1]
+            busy.clear()
             accsb = work.tile([P, BATCH * P], F32, name="accsb%d" % last, tag="accsb", bufs=2)
-            nc.vector.tensor_copy(out=accsb[:, lo * P : (hi + 1) * P], in_=sums[:, lo * P : (hi + 1) * P])
+            (nc.scalar.copy if FINS and last != LENTS[-1] else nc.vector.tensor_copy)(
+                out=accsb[:, lo * P : (hi + 1) * P], in_=sums[:, lo * P : (hi + 1) * P]
+            )
             for q in range(lo, hi + 1):
                 k = column(LENTS[LENTS.index(last) - (hi - q)])
                 nc.tensor.matmul(
@@ -398,16 +441,23 @@ def tile_fr_pa_kernel(tc, x1, x2, c1_w, c1_b, c2_w, c2_b, out_0, out_1):
 
         new_x(0, 0)
         new_x(0, 1)
+        if XFIRST:
+            regroup_v(0, 0)
+            regroup_s(0, 0)
         nc.vector.tensor_copy(out=bwide[0:8, :], in_=braw[:])
         w0 = transpose_w([0, 1], [0, 1])
         copy_w(w0)
-        regroup_v(0, 0)
-        regroup_s(0, 0)
+        if not XFIRST:
+            regroup_v(0, 0)
+            regroup_s(0, 0)
+        if XFIRST:
+            quant_x(0, 0, 0, HALF)
         quant_w([0, 1])
         prep_bias()
         regroup_v(0, 1)
         regroup_s(0, 1)
-        quant_x(0, 0, 0, HALF)
+        if not XFIRST:
+            quant_x(0, 0, 0, HALF)
         regroup_v(1, 0)
         regroup_s(1, 0)
         quant_x(0, 0, HALF, POS)
@@ -447,14 +497,34 @@ def tile_fr_pa_kernel(tc, x1, x2, c1_w, c1_b, c2_w, c2_b, out_0, out_1):
 
         def after_quant(n, c):
             held[0] = False
-            return
+            quota[0] = QUOTA if (n, c) != order[0] else 0
+            if GUARD:
+                k = order.index((n, c)) + 1
+                if k == len(order):
+                    fence[0] = FENCE
+                if k < len(order):
+                    piece(order[k][0], order[k][1], 0)
+                    issued[0] += 1
+                    if H1NOW:
+                        second(order[k])
+
+        quota = [0]
+
+        def second(nc_):
+            n, c = nc_
+            piece(n, c, 1)
+            issued[0] += 1
+            held[0] = HOLD
+            if (n, c) in LOADS:
+                load_x(*LOADS[(n, c)])
 
         pieces = [(n, c, h) for n, c in order for h in range(2)]
-        for k in range(HEADP):
+        for k in range(2 if GUARD else HEADP):
             piece(*pieces[k])
         load_x(2, 0)
-        load_x(2, 1)
-        issued = [HEADP]
+        if not GUARD:
+            load_x(2, 1)
+        issued = [2 if GUARD else HEADP]
         if W2LATE:
             stage_mm(2)
         w2 = transpose_w([4, 5], W2B)
@@ -473,6 +543,9 @@ def tile_fr_pa_kernel(tc, x1, x2, c1_w, c1_b, c2_w, c2_b, out_0, out_1):
 
         done = []
         folded = []
+        lastfold = [0]
+        prodstep = {}
+        foldstep = {}
         for i in range(NG + LAG):
             while spieces and (SX if spieces[0][0] > 1 else SX1) == 0:
                 spieces.pop(0)
@@ -488,18 +561,23 @@ def tile_fr_pa_kernel(tc, x1, x2, c1_w, c1_b, c2_w, c2_b, out_0, out_1):
                     stage_copy_max(i + COPY, (1,))
             if i >= LAG:
                 stage_c(i - LAG)
-                if i - LAG == NG - 1:
+                if i - LAG == NG - 1 and not SPLITC:
                     nc.vector.reciprocal(out=rec[:], in_=sume[:])
                 if (i - LAG) not in LENTS and i - LAG < NG - 1:
                     stage_d(i - LAG)
+            if i - LAG in PLS:
+                stage_prod(i - LAG)
             for g in LENTS:
-                if g + (PLAG if g < 24 else LAG) == i:
+                if g + (PLAG if g < 24 else LAG) == i and g not in PLS:
                     waiting.append(g)
             if LATE31 and i == NG - 4 + LAG:
                 stage_mm(NG - 1)
             if not held[0]:
-                while waiting:
-                    stage_prod(waiting.pop(0))
+                while waiting and len(prod) - len(folded) < PB and (quota[0] > 0 or not GUARD or issued[0] >= len(pieces)):
+                    g = waiting.pop(0)
+                    stage_prod(g)
+                    prodstep[g] = i
+                    quota[0] -= 1
             if i < NG:
                 if i > 0:
                     stage_a(i)
@@ -524,7 +602,11 @@ def tile_fr_pa_kernel(tc, x1, x2, c1_w, c1_b, c2_w, c2_b, out_0, out_1):
                 stage_copy_max(i + COPY, (1,))
             if not QHEAD:
                 quants(i)
-            while issued[0] < len(pieces) and G0 + GS * (issued[0] - HEADP) + GB * ((issued[0] - HEADP) // 4) <= i:
+            if GUARD and not H1NOW:
+                for nc_ in order[1:]:
+                    if i == qstep[nc_] - HL:
+                        second(nc_)
+            while not GUARD and issued[0] < len(pieces) and G0 + GS * (issued[0] - HEADP) + GB * ((issued[0] - HEADP) // 4) <= i:
                 n, c, h = pieces[issued[0]]
                 piece(n, c, h)
                 issued[0] += 1
@@ -539,13 +621,18 @@ def tile_fr_pa_kernel(tc, x1, x2, c1_w, c1_b, c2_w, c2_b, out_0, out_1):
             if 2 < i + EVEN < NG - (1 if LATE31 else 0) and not is_g(i + EVEN):
                 stage_mm(i + EVEN)
             for g in LENTS:
-                if g in folded and g not in done and slot(g) == BATCH - 1 and g != LENTS[-1]:
+                if g in folded and foldstep[g] + FIN <= i and g not in done and slot(g) == BATCH - 1 and g != LENTS[-1]:
                     stage_finish(g)
                     done.append(g)
             for g in LENTS:
-                if g + (PLAG + FOLD if g < 24 else LAG + FOLD2) <= i and g not in folded and g in prod and i < NG + LAG:
+                k = LENTS.index(g)
+                if g in prod and g not in folded and prodstep[g] + FOLD <= i and i > lastfold[0] and (k == 0 or slot(g) != 0 or LENTS[k - 1] in done):
+                    lastfold[0] = i
                     stage_fold(g)
                     folded.append(g)
+                    foldstep[g] = i
+        if SPLITC:
+            stage_d(NG - 1, (0,))
         for g in LENTS:
             if g not in folded:
                 if g not in prod:
@@ -554,9 +641,16 @@ def tile_fr_pa_kernel(tc, x1, x2, c1_w, c1_b, c2_w, c2_b, out_0, out_1):
             if (slot(g) == BATCH - 1 or g == LENTS[-1]) and g not in done:
                 stage_finish(g)
         part = keep.tile([P, NG], F32, name="part")
-        stage_d(NG - 1, (0,))
-        nc.vector.tensor_add(out=part[:], in0=sd[:, 0, :], in1=fin)
-        stage_d(NG - 1, (1,))
+        if SPLITC:
+            klast = column(NG - 1)
+            stage_d(NG - 1, (1,))
+            nc.vector.tensor_add(out=sume[:, klast : klast + 1], in0=sume[:, klast : klast + 1], in1=sumlast[:])
+            nc.vector.tensor_add(out=part[:], in0=sd[:, 0, :], in1=fin)
+            nc.vector.reciprocal(out=rec[:], in_=sume[:])
+        else:
+            stage_d(NG - 1, (0,))
+            nc.vector.tensor_add(out=part[:], in0=sd[:, 0, :], in1=fin)
+            stage_d(NG - 1, (1,))
 
         nc.vector.tensor_mul(out=part[:], in0=part[:], in1=rec[:])
         num = keep.tile([P, NG], F32, name="num")

@@ -21,8 +21,11 @@ NW = 2
 OT = 4
 NG = NB * NW * OT
 RUN = 4
+PST = (0, 2, 4, 6)
+TWO = True
+LASTEARLY = True
 FENCE = True
-QUOTA = 1
+QUOTA = 2
 H1NOW = False
 GUARD = True
 LASTFOLD = 33
@@ -38,15 +41,15 @@ GS = 2
 G0 = 4
 HEADP = 4
 G1B = (0, 1)
-QALL = (1, 4, 8, 12, 16, 20)
+QALL = (5, 5, 13, 13, 21, 21)
 LB2 = True
 FOLD2 = 1
 LATE31 = True
 HOLD = True
 C1EARLY = True
-LOADS = {(1, 1): (2, 1), (2, 0): (3, 0), (2, 1): (3, 1)}
+LOADS = {(2, 0): (3, 0), (2, 1): (3, 1)}
 HL = 1
-XGB = 1
+XGB = 2
 W1FIRST = True
 SPAR = 0
 SX1 = 0
@@ -68,7 +71,7 @@ AB = 4
 EVB = 2
 PB = 4
 YB = 8
-EGB = 8
+EGB = 7
 EVEN = 2
 GSTEPS = range(4, 32, 2)
 QSTEP = (3, 5)
@@ -81,7 +84,7 @@ LENT_BANKS = (0, 1)
 OWN_BANKS = (2, 3, 4, 5, 6)
 
 
-LSET = range(1, 30, 2)
+LSET = range(1, 28, 2)
 VLENTS = list(LSET)
 SLS = ()
 PLS = ()
@@ -228,7 +231,7 @@ def tile_fr_pa_kernel(tc, x1, x2, c1_w, c1_b, c2_w, c2_b, out_0, out_1):
 
         def new_x(n, c):
             xg[(n, c)] = work.tile(
-                [P, POS, PACK], BF16, name="xg%d%d" % (n, c), tag="xg" if n == 0 else "xh", bufs=2 if n == 0 else XGB, align_bytes=64
+                [P, POS, PACK], BF16, name="xg%d%d" % (n, c), tag="xg", bufs=XGB, align_bytes=64
             )
             if c == 0:
                 xq[n] = keep.tile([P, 2, POS], U32, name="xq%d" % n, align_bytes=64)
@@ -385,7 +388,7 @@ def tile_fr_pa_kernel(tc, x1, x2, c1_w, c1_b, c2_w, c2_b, out_0, out_1):
 
         def stage_prod(g):
             if fence[0]:
-                prod[g] = work.tile([P, POS], F32, name="prod%d" % g, tag="xh", bufs=XGB, align_bytes=64)
+                prod[g] = work.tile([P, POS], F32, name="prod%d" % g, tag="xg", bufs=XGB, align_bytes=64)
                 fence[0] = False
             else:
                 prod[g] = work.tile(
@@ -502,11 +505,33 @@ def tile_fr_pa_kernel(tc, x1, x2, c1_w, c1_b, c2_w, c2_b, out_0, out_1):
                 k = order.index((n, c)) + 1
                 if k == len(order):
                     fence[0] = FENCE
-                if k < len(order):
+                if k < len(order) and not TWO:
                     piece(order[k][0], order[k][1], 0)
                     issued[0] += 1
                     if H1NOW:
                         second(order[k])
+                if TWO and c == 1:
+                    base[0] = i0[0]
+                    quota[0] = QUOTA
+                    more()
+                if TWO and c == 0:
+                    held[0] = True
+
+        base = [None]
+        i0 = [0]
+
+        def more():
+            while base[0] is not None and issued[0] < len(pieces) and issued[0] // 4 == batch_of(base[0]) and base[0] + PST[issued[0] % 4] <= i0[0]:
+                n, c, h = pieces[issued[0]]
+                piece(n, c, h)
+                issued[0] += 1
+                if h == 1 and (n, c) in LOADS:
+                    load_x(*LOADS[(n, c)])
+                if c == 1 and h == 1:
+                    held[0] = HOLD
+
+        def batch_of(s):
+            return [qstep[(n, 1)] for n in range(1, NB)].index(s) + 1
 
         quota = [0]
 
@@ -519,12 +544,12 @@ def tile_fr_pa_kernel(tc, x1, x2, c1_w, c1_b, c2_w, c2_b, out_0, out_1):
                 load_x(*LOADS[(n, c)])
 
         pieces = [(n, c, h) for n, c in order for h in range(2)]
-        for k in range(2 if GUARD else HEADP):
+        for k in range(4 if TWO else 2 if GUARD else HEADP):
             piece(*pieces[k])
         load_x(2, 0)
-        if not GUARD:
+        if not GUARD or TWO:
             load_x(2, 1)
-        issued = [2 if GUARD else HEADP]
+        issued = [4 if TWO else 2 if GUARD else HEADP]
         if W2LATE:
             stage_mm(2)
         w2 = transpose_w([4, 5], W2B)
@@ -547,6 +572,7 @@ def tile_fr_pa_kernel(tc, x1, x2, c1_w, c1_b, c2_w, c2_b, out_0, out_1):
         prodstep = {}
         foldstep = {}
         for i in range(NG + LAG):
+            i0[0] = i
             while spieces and (SX if spieces[0][0] > 1 else SX1) == 0:
                 spieces.pop(0)
             if spieces and (i % 2 == SPAR or spieces[0][0] == 1):
@@ -602,7 +628,9 @@ def tile_fr_pa_kernel(tc, x1, x2, c1_w, c1_b, c2_w, c2_b, out_0, out_1):
                 stage_copy_max(i + COPY, (1,))
             if not QHEAD:
                 quants(i)
-            if GUARD and not H1NOW:
+            if TWO:
+                more()
+            if GUARD and not H1NOW and not TWO:
                 for nc_ in order[1:]:
                     if i == qstep[nc_] - HL:
                         second(nc_)
@@ -631,36 +659,40 @@ def tile_fr_pa_kernel(tc, x1, x2, c1_w, c1_b, c2_w, c2_b, out_0, out_1):
                     stage_fold(g)
                     folded.append(g)
                     foldstep[g] = i
-        if SPLITC:
-            stage_d(NG - 1, (0,))
-        for g in LENTS:
-            if g not in folded:
-                if g not in prod:
-                    stage_prod(g)
-                stage_fold(g)
-            if (slot(g) == BATCH - 1 or g == LENTS[-1]) and g not in done:
-                stage_finish(g)
-        part = keep.tile([P, NG], F32, name="part")
-        if SPLITC:
-            klast = column(NG - 1)
-            stage_d(NG - 1, (1,))
-            nc.vector.tensor_add(out=sume[:, klast : klast + 1], in0=sume[:, klast : klast + 1], in1=sumlast[:])
-            nc.vector.tensor_add(out=part[:], in0=sd[:, 0, :], in1=fin)
-            nc.vector.reciprocal(out=rec[:], in_=sume[:])
-        else:
-            stage_d(NG - 1, (0,))
-            nc.vector.tensor_add(out=part[:], in0=sd[:, 0, :], in1=fin)
-            stage_d(NG - 1, (1,))
-
-        nc.vector.tensor_mul(out=part[:], in0=part[:], in1=rec[:])
+        klast = column(NG - 1)
         num = keep.tile([P, NG], F32, name="num")
-        nc.vector.tensor_mul(out=num[:], in0=sd[:, 1, :], in1=rec[:])
+        part = keep.tile([P, NG], F32, name="part")
+        stage_d(NG - 1)
+        nc.vector.tensor_add(out=sume[:, klast : klast + 1], in0=sume[:, klast : klast + 1], in1=sumlast[:])
+        if LASTEARLY:
+            for g in LENTS:
+                if g not in folded:
+                    if g not in prod:
+                        stage_prod(g)
+                    stage_fold(g)
+                if (slot(g) == BATCH - 1 or g == LENTS[-1]) and g not in done:
+                    stage_finish(g)
+
+        nc.vector.tensor_add(out=num[:], in0=sd[:, 0, :], in1=sd[:, 1, :])
+        nc.vector.reciprocal(out=rec[:], in_=sume[:])
+        nc.vector.tensor_mul(out=num[:], in0=num[:], in1=rec[:])
         nc.vector.tensor_add(
-            out=part[:].rearrange("p (w n t) -> p w n t", w=NW, n=NB),
-            in0=part[:].rearrange("p (w n t) -> p w n t", w=NW, n=NB),
+            out=num[:].rearrange("p (w n t) -> p w n t", w=NW, n=NB),
+            in0=num[:].rearrange("p (w n t) -> p w n t", w=NW, n=NB),
             in1=bias[:].rearrange("p (w t) -> p w t", w=NW).unsqueeze(2).to_broadcast([P, NW, NB, OT]),
         )
+        if not LASTEARLY:
+            for g in LENTS:
+                if g not in folded:
+                    if g not in prod:
+                        stage_prod(g)
+                    stage_fold(g)
+                if (slot(g) == BATCH - 1 or g == LENTS[-1]) and g not in done:
+                    stage_finish(g)
+
+        nc.vector.tensor_mul(out=part[:], in0=rec[:], in1=fin)
         nc.vector.tensor_add(out=result[:, 0:NG], in0=num[:], in1=part[:])
+
         rt = bank(0, "rt")
         nc.tensor.transpose(out=rt[:, 0:P], in_=result[:], identity=ident[:])
         rows = keep.tile([P, P], F32, name="rows")

@@ -21,6 +21,12 @@ NW = 2
 OT = 4
 NG = NB * NW * OT
 RUN = 4
+XW = True
+EXTRA = (29,)
+KH = True
+NFOLD = 2
+Q0 = 1
+FIRST_BANKS = (2, 3, 4, 5, 6, 7)
 PST = (0, 2, 4, 6)
 TWO = True
 LASTEARLY = True
@@ -41,7 +47,7 @@ GS = 2
 G0 = 4
 HEADP = 4
 G1B = (0, 1)
-QALL = (5, 5, 13, 13, 21, 21)
+QALL = (5, 5, 12, 12, 20, 20)
 LB2 = True
 FOLD2 = 1
 LATE31 = True
@@ -58,7 +64,7 @@ W2B = [6, 7]
 W2LATE = False
 GQ = 1024
 GP = 1
-GP1 = 1
+GP1 = 2
 SUMS = 3
 W3B = [7, 6]
 W3V = 0
@@ -75,7 +81,7 @@ EGB = 7
 EVEN = 2
 GSTEPS = range(4, 32, 2)
 QSTEP = (3, 5)
-VSHARE = 296
+VSHARE = 256
 LAG = 2
 BATCH = 3
 FOLD = 2
@@ -146,6 +152,8 @@ def tile_fr_pa_kernel(tc, x1, x2, c1_w, c1_b, c2_w, c2_b, out_0, out_1):
             nc.sync.dma_start(out=xraw[(n, c)][:], in_=xsrc[c][n].rearrange("(p j) h w -> p j (h w)", j=PACK))
 
         def xhalf(n, c, h):
+            if XW:
+                return xraw[(n, c)][:, :, h * HALF : (h + 1) * HALF]
             return xraw[(n, c)][:].rearrange("p t w -> p (t w)")[:, h * PACK * HALF : (h + 1) * PACK * HALF].rearrange("p (t w) -> p t w", t=PACK)
 
         def load_x_half(n, c, h):
@@ -162,14 +170,18 @@ def tile_fr_pa_kernel(tc, x1, x2, c1_w, c1_b, c2_w, c2_b, out_0, out_1):
             src = (c1_w, c2_w)[w][lo * P : hi * P, :].rearrange("(t p) k -> p t k", p=P)
             nc.sync.dma_start(out=wraw[w][:, lo:hi, :], in_=src)
 
-        if XFIRST:
+        if XW and XFIRST:
+            load_x(0, 0)
+        elif XFIRST:
             load_x_half(0, 0, 0)
         load_w(0, 0, 2)
         nc.sync.dma_start(out=braw[0:4, :], in_=c1_b.rearrange("(t p) -> t p", p=P))
         nc.sync.dma_start(out=braw[4:8, :], in_=c2_b.rearrange("(t p) -> t p", p=P))
         for c in range(2):
+            if XW and (c == 1 or not XFIRST):
+                load_x(0, c)
             for h in range(2):
-                if not XFIRST or c + h > 0:
+                if not XW and (not XFIRST or c + h > 0):
                     load_x_half(0, c, h)
         load_w(0, 2, 4)
         load_w(1, 0, 4)
@@ -298,7 +310,7 @@ def tile_fr_pa_kernel(tc, x1, x2, c1_w, c1_b, c2_w, c2_b, out_0, out_1):
         def stage_mm(g, halves=(0, 1)):
             n, j = divmod(g, 8)
             for h in halves:
-                if is_g(g) or (LB2 and g == 29):
+                if is_g(g) or g in EXTRA:
                     b = G1B[h] if g == 1 else LENT_BANKS[h]
                 else:
                     b = OWN_BANKS[turn[0] % len(OWN_BANKS)]
@@ -500,7 +512,7 @@ def tile_fr_pa_kernel(tc, x1, x2, c1_w, c1_b, c2_w, c2_b, out_0, out_1):
 
         def after_quant(n, c):
             held[0] = False
-            quota[0] = QUOTA if (n, c) != order[0] else 0
+            quota[0] = QUOTA if (n, c) != order[0] else quota[0]
             if GUARD:
                 k = order.index((n, c)) + 1
                 if k == len(order):
@@ -533,7 +545,7 @@ def tile_fr_pa_kernel(tc, x1, x2, c1_w, c1_b, c2_w, c2_b, out_0, out_1):
         def batch_of(s):
             return [qstep[(n, 1)] for n in range(1, NB)].index(s) + 1
 
-        quota = [0]
+        quota = [Q0]
 
         def second(nc_):
             n, c = nc_

@@ -21,6 +21,7 @@ NW = 2
 OT = 4
 NG = NB * NW * OT
 RUN = 4
+SPLIT31 = False
 XW = True
 EXTRA = (29,)
 KH = True
@@ -184,8 +185,9 @@ def tile_fr_pa_kernel(tc, x1, x2, c1_w, c1_b, c2_w, c2_b, out_0, out_1):
                 if not XW and (not XFIRST or c + h > 0):
                     load_x_half(0, c, h)
         load_w(0, 2, 4)
-        load_w(1, 0, 4)
+        load_w(1, 0, 2)
         load_x(1, 0)
+        load_w(1, 2, 4)
 
         def wrow(j):
             return wraw[j // OT][:, j % OT, :].bitcast(F32)
@@ -609,7 +611,7 @@ def tile_fr_pa_kernel(tc, x1, x2, c1_w, c1_b, c2_w, c2_b, out_0, out_1):
                 if g + (PLAG if g < 24 else LAG) == i and g not in PLS:
                     waiting.append(g)
             if LATE31 and i == NG - 4 + LAG:
-                stage_mm(NG - 1)
+                stage_mm(NG - 1, (1,) if SPLIT31 else (0, 1))
             if not held[0]:
                 while waiting and len(prod) - len(folded) < PB and (quota[0] > 0 or not GUARD or issued[0] >= len(pieces)):
                     g = waiting.pop(0)
@@ -660,6 +662,8 @@ def tile_fr_pa_kernel(tc, x1, x2, c1_w, c1_b, c2_w, c2_b, out_0, out_1):
                 stage_mm(i + COPY + 1, (0, 1) if LB2 else (0,))
             if 2 < i + EVEN < NG - (1 if LATE31 else 0) and not is_g(i + EVEN):
                 stage_mm(i + EVEN)
+            if LATE31 and SPLIT31 and i + EVEN == NG - 1:
+                stage_mm(NG - 1, (0,))
             for g in LENTS:
                 if g in folded and foldstep[g] + FIN <= i and g not in done and slot(g) == BATCH - 1 and g != LENTS[-1]:
                     stage_finish(g)

from contextlib import ExitStack

import concourse.mybir as mybir
from concourse.masks import make_identity

F32 = mybir.dt.float32
BF16 = mybir.dt.bfloat16
U32 = mybir.dt.uint32
U8 = mybir.dt.uint8
FP8X4 = mybir.dt.float8_e4m3fn_x4
ACT = mybir.ActivationFunctionType
ALU = mybir.AluOpType
AX = mybir.AxisListType

P = 128
PACK = 4
NB = 4
POS = 1024
HALF = 512
NW = 2
OT = 4
NG = NB * NW * OT
RUN = 4
SPLIT31 = False
XW = True
EXTRA = (29,)
KH = True
NFOLD = 2
Q0 = 1
FIRST_BANKS = (2, 3, 4, 5, 6, 7)
PST = (0, 2, 4, 6)
TWO = True
LASTEARLY = True
FENCE = True
QUOTA = 2
H1NOW = False
GUARD = True
LASTFOLD = 33
KEEPHEAD = True
FB = 7
PVB = 2
XFIRST = False
SPLITC = True
FIN = 1
FINS = False
GB = 0
GS = 2
G0 = 4
HEADP = 4
G1B = (0, 1)
QALL = (5, 5, 12, 12, 20, 20)
LB2 = True
FOLD2 = 1
LATE31 = True
HOLD = True
C1EARLY = True
LOADS = {(2, 0): (3, 0), (2, 1): (3, 1)}
HL = 1
XGB = 2
W1FIRST = True
SPAR = 0
SX1 = 0
SX = 0
W2B = [6, 7]
W2LATE = False
GQ = 1024
GP = 1
GP1 = 2
SUMS = 3
W3B = [7, 6]
W3V = 0
W2V = 0
W1V = 0
WB = True
WQ = (1,2)
WC = (1,2)
AB = 4
EVB = 2
PB = 4
YB = 8
EGB = 7
EVEN = 2
GSTEPS = range(4, 32, 2)
QSTEP = (3, 5)
VSHARE = 256
LAG = 2
BATCH = 3
FOLD = 2
COPY = 2
LENT_BANKS = (0, 1)
OWN_BANKS = (2, 3, 4, 5, 6)


LSET = range(1, 28, 2)
VLENTS = list(LSET)
SLS = ()
PLS = ()
LENTS = sorted(VLENTS + list(SLS) + list(PLS))
PLAG = 2
QHEAD = False


def is_g(g):
    return g in VLENTS


FLOPS = 2 * NW * NB * 512 * 1024 * 1024


def tile_fr_pa_kernel(tc, x1, x2, c1_w, c1_b, c2_w, c2_b, out_0, out_1):
    nc = tc.nc
    xsrc = (x1, x2)
    with ExitStack() as ctx:
        keep = ctx.enter_context(tc.tile_pool(name="keep", bufs=1))
        work = ctx.enter_context(tc.tile_pool(name="work", bufs=3))
        psum = ctx.enter_context(tc.psum_pool(name="psum", bufs=1))
        ctx.enter_context(tc.manual_schedule())

        def bank(b, name):
            return psum.tile([P, HALF], F32, name=name, tag="bank%d" % b)

        ident = keep.tile([P, P], F32, name="ident")
        make_identity(nc, ident[:])
        warm_in = keep.tile([P, 1], F32, name="warm_in")
        warm_out = keep.tile([P, 1], F32, name="warm_out")
        nc.vector.memset(warm_in[:], 0.0)
        nc.scalar.activation(out=warm_out[:], in_=warm_in[:], func=ACT.Exp)
        braw = keep.tile([8, P], BF16, name="braw")
        bwide = keep.tile([P, P], F32, name="bwide")
        nc.vector.memset(bwide[:], 0.0)
        result = keep.tile([P, P], F32, name="result")
        nc.vector.memset(result[:], 0.0)
        negm = {}
        sume = keep.tile([P, NG], F32, name="sume")
        sd = keep.tile([P, 2, NG], F32, name="sd")
        nc.vector.memset(sd[:], 0.0)
        zeros = keep.tile([P, NG], F32, name="zeros")
        nc.vector.memset(zeros[:], 0.0)
        ones = keep.tile([P, 1], F32, name="ones")
        nc.vector.memset(ones[:], 1.0)
        sumlast = keep.tile([P, 1], F32, name="sumlast")
        junk = keep.tile([P, HALF], F32, name="junk")
        rec = keep.tile([P, NG], F32, name="rec")

        xraw = {}
        wraw = {}

        def big(name):
            return work.tile([P, PACK, POS], BF16, name=name, tag="raw", bufs=5)

        def load_x(n, c):
            xraw[(n, c)] = big("xraw%d%d" % (n, c))
            nc.sync.dma_start(out=xraw[(n, c)][:], in_=xsrc[c][n].rearrange("(p j) h w -> p j (h w)", j=PACK))

        def xhalf(n, c, h):
            if XW:
                return xraw[(n, c)][:, :, h * HALF : (h + 1) * HALF]
            return xraw[(n, c)][:].rearrange("p t w -> p (t w)")[:, h * PACK * HALF : (h + 1) * PACK * HALF].rearrange("p (t w) -> p t w", t=PACK)

        def load_x_half(n, c, h):
            if h == 0:
                xraw[(n, c)] = big("xraw%d%d" % (n, c))
            nc.sync.dma_start(
                out=xhalf(n, c, h),
                in_=xsrc[c][n].rearrange("(p j) h w -> p j (h w)", j=PACK)[:, :, h * HALF : (h + 1) * HALF],
            )

        def load_w(w, lo, hi):
            if lo == 0:
                wraw[w] = big("wraw%d" % w)
            src = (c1_w, c2_w)[w][lo * P : hi * P, :].rearrange("(t p) k -> p t k", p=P)
            nc.sync.dma_start(out=wraw[w][:, lo:hi, :], in_=src)

        if XW and XFIRST:
            load_x(0, 0)
        elif XFIRST:
            load_x_half(0, 0, 0)
        load_w(0, 0, 2)
        nc.sync.dma_start(out=braw[0:4, :], in_=c1_b.rearrange("(t p) -> t p", p=P))
        nc.sync.dma_start(out=braw[4:8, :], in_=c2_b.rearrange("(t p) -> t p", p=P))
        for c in range(2):
            if XW and (c == 1 or not XFIRST):
                load_x(0, c)
            for h in range(2):
                if not XW and (not XFIRST or c + h > 0):
                    load_x_half(0, c, h)
        load_w(0, 2, 4)
        load_w(1, 0, 2)
        load_x(1, 0)
        load_w(1, 2, 4)

        def wrow(j):
            return wraw[j // OT][:, j % OT, :].bitcast(F32)

        wq = {}
        ws = {}

        def transpose_w(tiles, banks):
            turned = []
            for j, b in zip(tiles, banks):
                words = wrow(j)
                wt = bank(b, "wt%d" % j)
                for c in range(2):
                    for u in range(2):
                        q = 2 * c + u
                        nc.tensor.transpose(
                            out=wt[:, q * P : (q + 1) * P],
                            in_=words[:, 256 * c + u : 256 * c + 256 : 2],
                            identity=ident[:],
                        )
                turned.append(wt)
            return tiles, turned

        gw = {}

        def copy_w(prepared, nv=0):
            tiles, turned = prepared
            nt = len(tiles)
            gw[tiles[0]] = work.tile([P, nt * 1024], BF16, name="gw%d" % tiles[0], tag="gw", bufs=2, align_bytes=64)
            for i, j in enumerate(tiles):
                (nc.vector.tensor_copy if i < nv else nc.scalar.copy)(
                    out=gw[tiles[0]][:, i * 1024 : (i + 1) * 1024].bitcast(F32).rearrange("p (c o u) -> p c o u", c=2, u=2),
                    in_=turned[i][:].rearrange("p (c u o) -> p c o u", c=2, u=2),
                )

        def quant_w(tiles):
            nt = len(tiles)
            codes = keep.tile([P, nt * 256], U32, name="wq%d" % tiles[0], align_bytes=64)
            plane = keep.tile([P, nt * 256], U8, name="ws%d" % tiles[0], align_bytes=64)
            for i, j in enumerate(tiles):
                wq[j] = codes[:, i * 256 : (i + 1) * 256]
                ws[j] = plane[:, i * 256 : (i + 1) * 256]
            nc.vector.quantize_mx(out=codes[:].bitcast(FP8X4), scales=plane[:], in_=gw[tiles[0]][:])

        bias = keep.tile([P, 8], F32, name="bias")

        def prep_bias():
            bt = bank(2, "bt")
            nc.tensor.transpose(out=bt[:, 0:P], in_=bwide[:], identity=ident[:])
            nc.vector.tensor_copy(out=bias[:], in_=bt[:, 0:8])

        xq = {}
        xs = {}
        xg = {}

        def new_x(n, c):
            xg[(n, c)] = work.tile(
                [P, POS, PACK], BF16, name="xg%d%d" % (n, c), tag="xg", bufs=XGB, align_bytes=64
            )
            if c == 0:
                xq[n] = keep.tile([P, 2, POS], U32, name="xq%d" % n, align_bytes=64)
                xs[n] = keep.tile([P, 2, POS], U8, name="xs%d" % n, align_bytes=64)

        def views(n, c, lo, hi):
            dst = xg[(n, c)][:, lo:hi, :].rearrange("p (q i) t -> p q t i", i=RUN)
            src = xhalf(n, c, lo // HALF)[:, :, lo % HALF : (hi - 1) % HALF + 1].rearrange("p t (q i) -> p q t i", i=RUN)
            return dst, src

        ready = {}

        def quant_x(n, c, lo, hi):
            assert n == 0 or ready[(n, c)] == 2048 * 1, (n, c, ready)
            nc.vector.quantize_mx(
                out=xq[n][:, c, lo:hi].bitcast(FP8X4),
                scales=xs[n][:, c, lo:hi],
                in_=xg[(n, c)][:, lo:hi, :].rearrange("p w t -> p (w t)"),
            )

        def regroup_v(c, h):
            dst, src = views(0, c, h * HALF, h * HALF + VSHARE)
            nc.vector.tensor_copy(out=dst, in_=src)

        def regroup_s(c, h):
            dst, src = views(0, c, h * HALF + VSHARE, (h + 1) * HALF)
            nc.scalar.copy(out=dst, in_=src)

        def regroup_gpsimd(n, c, h):
            end = (h + 1) * HALF - (SX1 if n == 1 else SX)
            ready[(n, c)] = ready.get((n, c), 0) + 2 * (end - h * HALF)
            gp = (end - h * HALF) // (GP1 if n == 1 else GP)
            for lo in range(h * HALF, end, gp):
                nc.gpsimd.tensor_scalar(
                    out=xg[(n, c)][:, lo : lo + gp, :],
                    in0=xraw[(n, c)][:, :, lo : lo + gp].rearrange("p t w -> p w t"),
                    scalar1=1.0,
                    scalar2=0.0,
                    op0=ALU.mult,
                    op1=ALU.add,
                )

        def regroup_sx(n, c, h):
            sx = SX1 if n == 1 else SX
            if sx == 0:
                return
            lo, hi = (h + 1) * HALF - sx, (h + 1) * HALF
            ready[(n, c)] = ready.get((n, c), 0) + 2 * sx
            dst = xg[(n, c)][:, lo:hi, :].rearrange("p (q i) t -> p q t i", i=RUN)
            src = xraw[(n, c)][:, :, lo:hi].rearrange("p t (q i) -> p q t i", i=RUN)
            nc.scalar.copy(out=dst, in_=src)

        ybank = {}
        ysb = {}
        prod = {}
        atile = {}
        etile = {}
        turn = [0]

        def column(g):
            n, j = divmod(g, 8)
            return (j // OT) * (NB * OT) + n * OT + j % OT

        def stage_mm(g, halves=(0, 1)):
            n, j = divmod(g, 8)
            for h in halves:
                if is_g(g) or g in EXTRA:
                    b = G1B[h] if g == 1 else LENT_BANKS[h]
                else:
                    b = OWN_BANKS[turn[0] % len(OWN_BANKS)]
                    turn[0] += 1
                ybank[(g, h)] = bank(b, "y%d_%d" % (g, h))
                for c in range(2):
                    nc.tensor.matmul_mx(
                        out=ybank[(g, h)][:],
                        lhsT=wq[j][:, c * P : (c + 1) * P].bitcast(FP8X4),
                        lhsT_scale=ws[j][:, c * P : (c + 1) * P],
                        rhs=xq[n][:, c, h * HALF : (h + 1) * HALF].bitcast(FP8X4),
                        rhs_scale=xs[n][:, c, h * HALF : (h + 1) * HALF],
                        start=(c == 0),
                        stop=(c == 1),
                    )

        def stage_copy_max(g, halves=(0, 1)):
            if 0 in halves:
                ysb[g] = work.tile([P, POS + 2], F32, name="ysb%d" % g, tag="ysb", bufs=YB)
            for h in halves:
                nc.vector.tensor_scalar(
                    out=ysb[g][:, h * HALF : (h + 1) * HALF],
                    in0=ybank[(g, h)][:],
                    scalar1=1.0,
                    scalar2=None,
                    op0=ALU.mult,
                    op1=ALU.max,
                    accum_out=ysb[g][:, POS + h : POS + h + 1],
                )

        def stage_a(g, halves=(0, 1)):
            j = g % 8
            if g not in atile:
                atile[g] = work.tile([P, POS + 2], F32, name="a%d" % g, tag="a", bufs=AB)
            if is_g(g):
                nc.scalar.activation(out=atile[g][:], in_=ysb[g][:], func=ACT.Exp, bias=bias[:, j : j + 1], scale=1.0)
                return
            for h in halves:
                nc.scalar.activation(
                    out=atile[g][:, h * HALF : (h + 1) * HALF],
                    in_=ybank[(g, h)][:],
                    func=ACT.Exp,
                    bias=bias[:, j : j + 1],
                    scale=1.0,
                )

        def stage_scopy(g):
            ysb[g] = work.tile([P, POS + 2], F32, name="ysb%d" % g, tag="ysb", bufs=YB)
            for h in range(2):
                nc.scalar.copy(out=ysb[g][:, h * HALF : (h + 1) * HALF], in_=ybank[(g, h)][:])

        def stage_b(g):
            negm[g] = work.tile([P, 1], F32, name="negm%d" % g, tag="negm", bufs=6)
            src = atile[g][:, POS : POS + 2] if is_g(g) else atile[g][:, 0:POS]
            nc.vector.tensor_reduce(out=negm[g][:], in_=src, axis=AX.X, op=ALU.max, negate=True)

        def stage_c(g):
            k = column(g)
            if g in LENTS and g not in PLS:
                etile[g] = work.tile([P, POS], F32, name="e%d" % g, tag="eg", bufs=EGB)
            else:
                etile[g] = work.tile([P, POS], F32, name="e%d" % g, tag="ev", bufs=EVB)
            for h, (lo, hi) in enumerate(((0, HALF), (HALF, POS)) if g == NG - 1 and SPLITC else ((0, POS),)):
                nc.scalar.activation(
                    out=etile[g][:, lo:hi],
                    in_=atile[g][:, lo:hi],
                    func=ACT.Exp,
                    bias=negm[g][:],
                    scale=1.0,
                    accum_out=sume[:, k : k + 1] if h == 0 else sumlast[:],
                )

        def stage_d(g, halves=(0, 1)):
            k = column(g)
            for h in halves:
                nc.vector.scalar_tensor_tensor(
                    out=junk[:],
                    in0=ybank[(g, h)][:],
                    scalar=1.0,
                    in1=etile[g][:, h * HALF : (h + 1) * HALF],
                    op0=ALU.mult,
                    op1=ALU.mult,
                    accum_out=sd[:, h, k : k + 1],
                )

        fence = [False]

        def stage_prod(g):
            if fence[0]:
                prod[g] = work.tile([P, POS], F32, name="prod%d" % g, tag="xg", bufs=XGB, align_bytes=64)
                fence[0] = False
            else:
                prod[g] = work.tile(
                    [P, POS], F32, name="prod%d" % g, tag="prodv" if g in PLS else "prod", bufs=PVB if g in PLS else PB
                )
            if g in PLS:
                for h in range(2):
                    nc.vector.tensor_tensor(
                        out=prod[g][:, h * HALF : (h + 1) * HALF],
                        in0=ybank[(g, h)][:],
                        in1=etile[g][:, h * HALF : (h + 1) * HALF],
                        op=ALU.mult,
                    )
                return
            for lo in range(0, POS, GQ):
                nc.gpsimd.tensor_tensor(
                    out=prod[g][:, lo : lo + GQ], in0=etile[g][:, lo : lo + GQ], in1=ysb[g][:, lo : lo + GQ], op=ALU.mult
                )

        def slot(g):
            return (LENTS.index(g) - len(LENTS) + 1) % BATCH

        busy = {}

        def stage_fold(g):
            q = slot(g)
            assert q not in busy and (q == 0 or LENTS[LENTS.index(g) - 1] in busy.values() or g == LENTS[0]), (g, busy)
            busy[q] = g
            for blk in range(POS // P):
                nc.tensor.matmul(
                    out=sums[:, q * P : (q + 1) * P],
                    lhsT=prod[g][:, blk * P : (blk + 1) * P],
                    rhs=ident[:],
                    is_transpose=True,
                    start=(blk == 0),
                    stop=(blk == POS // P - 1),
                )

        def stage_finish(last):
            hi = slot(last)
            lo = max(0, hi - LENTS.index(last))
            assert [busy[q] for q in range(lo, hi + 1)] == LENTS[LENTS.index(last) - (hi - lo) : LENTS.index(last) + 1]
            busy.clear()
            accsb = work.tile([P, BATCH * P], F32, name="accsb%d" % last, tag="accsb", bufs=2)
            (nc.scalar.copy if FINS and last != LENTS[-1] else nc.vector.tensor_copy)(
                out=accsb[:, lo * P : (hi + 1) * P], in_=sums[:, lo * P : (hi + 1) * P]
            )
            for q in range(lo, hi + 1):
                k = column(LENTS[LENTS.index(last) - (hi - q)])
                nc.tensor.matmul(
                    out=fin[:, k : k + 1], lhsT=accsb[:, q * P : (q + 1) * P], rhs=ones[:], start=True, stop=True
                )

        new_x(0, 0)
        new_x(0, 1)
        if XFIRST:
            regroup_v(0, 0)
            regroup_s(0, 0)
        nc.vector.tensor_copy(out=bwide[0:8, :], in_=braw[:])
        w0 = transpose_w([0, 1], [0, 1])
        copy_w(w0)
        if not XFIRST:
            regroup_v(0, 0)
            regroup_s(0, 0)
        if XFIRST:
            quant_x(0, 0, 0, HALF)
        quant_w([0, 1])
        prep_bias()
        regroup_v(0, 1)
        regroup_s(0, 1)
        if not XFIRST:
            quant_x(0, 0, 0, HALF)
        regroup_v(1, 0)
        regroup_s(1, 0)
        quant_x(0, 0, HALF, POS)
        regroup_v(1, 1)
        quant_x(0, 1, 0, HALF)
        w1 = transpose_w([2, 3], [6, 7])
        stage_mm(0, (0,))
        regroup_s(1, 1)
        if W1FIRST:
            copy_w(w1, W1V)
        stage_a(0, (0,))
        quant_x(0, 1, HALF, POS)
        stage_mm(0, (1,))
        stage_mm(1)
        if W1FIRST:
            quant_w([2, 3])
        stage_copy_max(1)
        stage_a(0, (1,))
        if not W1FIRST:
            copy_w(w1, W1V)
        stage_b(0)
        if not W1FIRST:
            quant_w([2, 3])
        load_x(1, 1)
        spieces = []
        order = [(n, c) for n in range(1, NB) for c in range(2)]
        qstep = {(n, c): QALL[2 * (n - 1) + c] for n, c in order}

        def piece(n, c, h):
            if h == 0:
                new_x(n, c)
            regroup_gpsimd(n, c, h)
            spieces.append((n, c, h))

        waiting = []
        held = [False]

        def after_quant(n, c):
            held[0] = False
            quota[0] = QUOTA if (n, c) != order[0] else quota[0]
            if GUARD:
                k = order.index((n, c)) + 1
                if k == len(order):
                    fence[0] = FENCE
                if k < len(order) and not TWO:
                    piece(order[k][0], order[k][1], 0)
                    issued[0] += 1
                    if H1NOW:
                        second(order[k])
                if TWO and c == 1:
                    base[0] = i0[0]
                    quota[0] = QUOTA
                    more()
                if TWO and c == 0:
                    held[0] = True

        base = [None]
        i0 = [0]

        def more():
            while base[0] is not None and issued[0] < len(pieces) and issued[0] // 4 == batch_of(base[0]) and base[0] + PST[issued[0] % 4] <= i0[0]:
                n, c, h = pieces[issued[0]]
                piece(n, c, h)
                issued[0] += 1
                if h == 1 and (n, c) in LOADS:
                    load_x(*LOADS[(n, c)])
                if c == 1 and h == 1:
                    held[0] = HOLD

        def batch_of(s):
            return [qstep[(n, 1)] for n in range(1, NB)].index(s) + 1

        quota = [Q0]

        def second(nc_):
            n, c = nc_
            piece(n, c, 1)
            issued[0] += 1
            held[0] = HOLD
            if (n, c) in LOADS:
                load_x(*LOADS[(n, c)])

        pieces = [(n, c, h) for n, c in order for h in range(2)]
        for k in range(4 if TWO else 2 if GUARD else HEADP):
            piece(*pieces[k])
        load_x(2, 0)
        if not GUARD or TWO:
            load_x(2, 1)
        issued = [4 if TWO else 2 if GUARD else HEADP]
        if W2LATE:
            stage_mm(2)
        w2 = transpose_w([4, 5], W2B)
        if not W2LATE:
            stage_mm(2)
        sums = None


        def quants(i):
            for n, c in order:
                if i == qstep[(n, c)]:
                    while spieces and spieces[0][:2] == (n, c) and (SX1 if n == 1 else SX):
                        regroup_sx(*spieces.pop(0))
                    quant_x(n, c, 0, POS)
                    after_quant(n, c)

        done = []
        folded = []
        lastfold = [0]
        prodstep = {}
        foldstep = {}
        for i in range(NG + LAG):
            i0[0] = i
            while spieces and (SX if spieces[0][0] > 1 else SX1) == 0:
                spieces.pop(0)
            if spieces and (i % 2 == SPAR or spieces[0][0] == 1):
                regroup_sx(*spieces.pop(0))
            if QHEAD:
                quants(i)
            if is_g(i + COPY) and i + COPY > 1:
                stage_copy_max(i + COPY, (0,))
                if not LB2:
                    stage_mm(i + COPY, (1,))
                if C1EARLY:
                    stage_copy_max(i + COPY, (1,))
            if i >= LAG:
                stage_c(i - LAG)
                if i - LAG == NG - 1 and not SPLITC:
                    nc.vector.reciprocal(out=rec[:], in_=sume[:])
                if (i - LAG) not in LENTS and i - LAG < NG - 1:
                    stage_d(i - LAG)
            if i - LAG in PLS:
                stage_prod(i - LAG)
            for g in LENTS:
                if g + (PLAG if g < 24 else LAG) == i and g not in PLS:
                    waiting.append(g)
            if LATE31 and i == NG - 4 + LAG:
                stage_mm(NG - 1, (1,) if SPLIT31 else (0, 1))
            if not held[0]:
                while waiting and len(prod) - len(folded) < PB and (quota[0] > 0 or not GUARD or issued[0] >= len(pieces)):
                    g = waiting.pop(0)
                    stage_prod(g)
                    prodstep[g] = i
                    quota[0] -= 1
            if i < NG:
                if i > 0:
                    stage_a(i)
                if i in SLS:
                    stage_scopy(i)
                if i == WC[0]:
                    copy_w(w2, W2V)
                    w3 = transpose_w([6, 7], W3B)
                if i == WC[1]:
                    copy_w(w3, W3V)
                if i == WQ[0] and not WB:
                    quant_w([4, 5])
                if i == WQ[1] and not WB:
                    quant_w([6, 7])
                if i > 0:
                    stage_b(i)
                if i == WQ[0] and WB:
                    quant_w([4, 5])
                if i == WQ[1] and WB:
                    quant_w([6, 7])
            if is_g(i + COPY) and i + COPY > 1 and not C1EARLY:
                stage_copy_max(i + COPY, (1,))
            if not QHEAD:
                quants(i)
            if TWO:
                more()
            if GUARD and not H1NOW and not TWO:
                for nc_ in order[1:]:
                    if i == qstep[nc_] - HL:
                        second(nc_)
            while not GUARD and issued[0] < len(pieces) and G0 + GS * (issued[0] - HEADP) + GB * ((issued[0] - HEADP) // 4) <= i:
                n, c, h = pieces[issued[0]]
                piece(n, c, h)
                issued[0] += 1
                if h == 1 and (n, c) in LOADS:
                    load_x(*LOADS[(n, c)])
            if i == SUMS:
                sums = bank(7, "sums")
                fin = sums[:, BATCH * P : BATCH * P + NG]
                nc.tensor.matmul(out=fin, lhsT=ident[:], rhs=zeros[:], start=True, stop=True)
            if is_g(i + COPY + 1) and i + COPY + 1 > 1:
                stage_mm(i + COPY + 1, (0, 1) if LB2 else (0,))
            if 2 < i + EVEN < NG - (1 if LATE31 else 0) and not is_g(i + EVEN):
                stage_mm(i + EVEN)
            if LATE31 and SPLIT31 and i + EVEN == NG - 1:
                stage_mm(NG - 1, (0,))
            for g in LENTS:
                if g in folded and foldstep[g] + FIN <= i and g not in done and slot(g) == BATCH - 1 and g != LENTS[-1]:
                    stage_finish(g)
                    done.append(g)
            for g in LENTS:
                k = LENTS.index(g)
                if g in prod and g not in folded and prodstep[g] + FOLD <= i and i > lastfold[0] and (k == 0 or slot(g) != 0 or LENTS[k - 1] in done):
                    lastfold[0] = i
                    stage_fold(g)
                    folded.append(g)
                    foldstep[g] = i
        klast = column(NG - 1)
        num = keep.tile([P, NG], F32, name="num")
        part = keep.tile([P, NG], F32, name="part")
        stage_d(NG - 1)
        nc.vector.tensor_add(out=sume[:, klast : klast + 1], in0=sume[:, klast : klast + 1], in1=sumlast[:])
        if LASTEARLY:
            for g in LENTS:
                if g not in folded:
                    if g not in prod:
                        stage_prod(g)
                    stage_fold(g)
                if (slot(g) == BATCH - 1 or g == LENTS[-1]) and g not in done:
                    stage_finish(g)

        nc.vector.tensor_add(out=num[:], in0=sd[:, 0, :], in1=sd[:, 1, :])
        nc.vector.reciprocal(out=rec[:], in_=sume[:])
        nc.vector.tensor_mul(out=num[:], in0=num[:], in1=rec[:])
        nc.vector.tensor_add(
            out=num[:].rearrange("p (w n t) -> p w n t", w=NW, n=NB),
            in0=num[:].rearrange("p (w n t) -> p w n t", w=NW, n=NB),
            in1=bias[:].rearrange("p (w t) -> p w t", w=NW).unsqueeze(2).to_broadcast([P, NW, NB, OT]),
        )
        if not LASTEARLY:
            for g in LENTS:
                if g not in folded:
                    if g not in prod:
                        stage_prod(g)
                    stage_fold(g)
                if (slot(g) == BATCH - 1 or g == LENTS[-1]) and g not in done:
                    stage_finish(g)

        nc.vector.tensor_mul(out=part[:], in0=rec[:], in1=fin)
        nc.vector.tensor_add(out=result[:, 0:NG], in0=num[:], in1=part[:])

        rt = bank(0, "rt")
        nc.tensor.transpose(out=rt[:, 0:P], in_=result[:], identity=ident[:])
        rows = keep.tile([P, P], F32, name="rows")
        nc.vector.tensor_copy(out=rows[:], in_=rt[:, 0:P])
        nc.sync.dma_start(out=out_0.rearrange("n (t p) -> (n t) p", p=P), in_=rows[0:16, :])
        nc.sync.dma_start(out=out_1.rearrange("n (t p) -> (n t) p", p=P), in_=rows[16:32, :])
